import numpy as np
import ml_dtypes


def mxq(x, axis, fmt="e4m3"):
    dtype, down = {"e4m3": (ml_dtypes.float8_e4m3fn, 7), "e5m2": (ml_dtypes.float8_e5m2, 14)}[fmt]
    v = np.moveaxis(np.asarray(x, np.float32).astype(ml_dtypes.bfloat16).astype(np.float64), axis, -1)
    blocks = v.reshape(v.shape[:-1] + (-1, 32))
    amax = np.abs(blocks).max(-1, keepdims=True)
    byte = np.maximum(np.where(amax > 0, np.frexp(amax)[1] - 1 + 127, 0) - down, 1)
    scale = np.exp2(byte - 127.0)
    codes = (blocks / scale).astype(np.float32).astype(dtype).astype(np.float64)
    return np.moveaxis((codes * scale).reshape(v.shape), -1, axis)


WIDE = False


def mx_kscale(k):
    if not WIDE:
        return np.ones(k)
    levels = np.array([10, -10, 5, -5, 0])
    if k % 512:
        return np.exp2(np.random.permutation(np.resize(levels, k // 32))).repeat(32)
    a = np.empty((k // 512, 16))
    for p in range(k // 512):
        a[p, :8] = np.random.permutation(np.resize(levels, 8))
        for g in range(8):
            far = levels[np.abs(levels - a[p, g]) >= 10]
            a[p, g + 8] = far[np.random.randint(len(far))]
    return np.exp2(a.ravel()).repeat(32)


BF16 = ml_dtypes.bfloat16


def bf(x):
    return np.asarray(x, np.float32).astype(BF16)


def f64(x):
    return np.asarray(x).astype(np.float64)


B, NT, N, C, DV, TM = 2, 128, 512, 1024, 1024, 128


def softmax(s):
    e = np.exp(s - s.max(-1, keepdims=True))
    return e / e.sum(-1, keepdims=True)


def setup_inputs():
    s = mx_kscale(C)
    q = np.random.standard_normal((B, 1, C)) + np.random.standard_normal((B, NT, C))
    k = bf(np.random.standard_normal((B, N, C)) * 1.4)
    ki = bf(np.random.standard_normal((B, N, C)) * 1.4)
    ki[-1] = k[-1]
    return {'q': bf(q), 'k': k, 'ki': ki,
            'xs': bf(np.random.standard_normal((B, N, C)) * s),
            'xis': bf(np.random.standard_normal((B, N, C)) * s),
            'Wv': bf(np.random.standard_normal((C, DV)) * 1.8 / np.sqrt(C) / s[:, None])}


def reference(q, k, ki, xs, xis, Wv):
    scale = C ** -0.5
    aw = softmax(f64(q) @ f64(k).transpose(0, 2, 1) * scale)
    awi = softmax(f64(q) @ f64(ki).transpose(0, 2, 1) * scale)
    D = aw - awi
    ones_cnt = np.where(D > 0, 1.0, 0.0).sum(axis=1)
    half_cnt = np.where(D == 0, 1.0, 0.0).sum(axis=1)
    rgb_ratio = (ones_cnt / NT)[..., None]
    eq_ratio = (half_cnt / NT)[..., None]
    tir_ratio = 1.0 - rgb_ratio - eq_ratio
    wv = mxq(f64(Wv), 0, 'e4m3')
    v = mxq(f64(xs), 2, 'e4m3') @ wv
    vi = mxq(f64(xis), 2, 'e4m3') @ wv
    return v * (rgb_ratio + eq_ratio) + vi * (tir_ratio + eq_ratio)

@@ -1,0 +1,313 @@
+from contextlib import ExitStack
+
+import concourse.mybir as mybir
+from concourse.masks import make_identity
+
+BF16 = mybir.dt.bfloat16
+F32 = mybir.dt.float32
+U32 = mybir.dt.uint32
+U8 = mybir.dt.uint8
+FP8X4 = mybir.dt.float8_e4m3fn_x4
+ALU = mybir.AluOpType
+ACT = mybir.ActivationFunctionType
+AXIS = mybir.AxisListType
+
+P = 128
+BATCH = 2
+QUERIES = 128
+KEYS = 512
+C = 1024
+DV = 1024
+KEY_TILES = KEYS // P
+PAIR = 2
+WORD_CHUNKS = C // PAIR // P
+PACK = 4
+PASSES = C // (P * PACK)
+BANK = 512
+DV_HALVES = DV // BANK
+COUNT_COLS = 32
+UNIT_BANKS = 4
+SHARED_VECTOR_BANKS = 1
+SCALE = C**-0.5
+
+FLOPS = 2 * BATCH * 2 * QUERIES * KEYS * C + 2 * BATCH * 2 * KEYS * C * DV
+
+
+def tile_crossattention_for_fusion_temporal_pa_kernel(tc, q, k, ki, xs, xis, Wv, out):
+    nc = tc.nc
+    with ExitStack() as ctx:
+        resident = ctx.enter_context(tc.tile_pool(name="resident", bufs=1))
+        rotating = ctx.enter_context(tc.tile_pool(name="rotating", bufs=2))
+        small = ctx.enter_context(tc.tile_pool(name="small", bufs=4))
+        psum = ctx.enter_context(tc.psum_pool(name="psum", bufs=8))
+        ctx.enter_context(tc.manual_schedule())
+
+        w_raw = resident.tile([P, PASSES * PACK * DV], BF16, name="w_raw")
+        for g in range(PASSES):
+            rows = Wv[g * P * PACK : (g + 1) * P * PACK, :]
+            nc.sync.dma_start(
+                out=w_raw[:, g * PACK * DV : (g + 1) * PACK * DV],
+                in_=rows.rearrange("(p t) d -> p (t d)", t=PACK),
+            )
+
+        q_sb = resident.tile([P, BATCH * C], BF16, name="q_sb")
+        nc.sync.dma_start(
+            out=q_sb[:].rearrange("p (b c) -> p b c", b=BATCH), in_=q.rearrange("b r c -> r b c")
+        )
+
+        def load_rows(name, rows):
+            rows_sb = resident.tile([P, KEY_TILES * C], BF16, name=name)
+            nc.sync.dma_start(out=rows_sb[:], in_=rows.rearrange("(p j) c -> p (j c)", j=KEY_TILES))
+            return rows_sb
+
+        keys_sb = [
+            load_rows("keys_sb%d%d" % (b, stream), rows[b])
+            for b in range(BATCH)
+            for stream, rows in enumerate((k, ki))
+        ]
+        tokens_sb = [
+            load_rows("tokens_sb%d%d" % (b, stream), rows[b])
+            for b in range(BATCH)
+            for stream, rows in enumerate((xs, xis))
+        ]
+
+        ident = resident.tile([P, P], F32, name="ident")
+        make_identity(nc, ident[:])
+        vote_share = resident.tile([P, COUNT_COLS], BF16, name="vote_share")
+        nc.vector.memset(vote_share[:], 1.0 / QUERIES)
+        zero = small.tile([P, 1], F32, tag="zero")
+        nc.vector.memset(zero[:], 0.0)
+        one = small.tile([P, 1], F32, tag="one")
+        nc.scalar.activation(out=one[:], in_=zero[:], func=ACT.Exp)
+
+        w_grouped = resident.tile([P, PASSES * DV * PACK], BF16, name="w_grouped", align_bytes=64)
+        w_codes = resident.tile([P, PASSES * DV], U32, name="w_codes", align_bytes=64)
+        w_scales = resident.tile([P, PASSES * DV], U8, name="w_scales", align_bytes=64)
+        raw_view = w_raw[:].rearrange("p (g t d) -> p g t d", g=PASSES, t=PACK)
+        grouped_view = w_grouped[:].rearrange("p (g d t) -> p g d t", g=PASSES, t=PACK)
+        for g in range(PASSES):
+            for h in range(DV_HALVES):
+                cols = slice(h * BANK, (h + 1) * BANK)
+                nc.vector.tensor_copy(
+                    out=grouped_view[:, g, cols, :].rearrange("p (c i) t -> p c t i", i=4),
+                    in_=raw_view[:, g, :, cols].rearrange("p t (c i) -> p c t i", i=4),
+                )
+        for g in range(PASSES):
+            nc.vector.quantize_mx(
+                out=w_codes[:, g * DV : (g + 1) * DV].bitcast(FP8X4),
+                scales=w_scales[:, g * DV : (g + 1) * DV],
+                in_=w_grouped[:, g * DV * PACK : (g + 1) * DV * PACK],
+            )
+
+        def transpose_words(bank_cols, words):
+            nc.tensor.transpose(bank_cols, words, ident[:])
+
+        qT = resident.tile([P, BATCH * PAIR * BANK], BF16, name="qT")
+        q_words = q_sb[:].bitcast(F32)
+        for b in range(BATCH):
+            q_bank = psum.tile([P, BANK], F32, tag="bank")
+            for g in range(WORD_CHUNKS):
+                first = (b * WORD_CHUNKS + g) * P
+                transpose_words(q_bank[:, g * P : (g + 1) * P], q_words[:, first : first + P])
+            nc.scalar.copy(
+                out=qT[:, b * PAIR * BANK : (b + 1) * PAIR * BANK], in_=q_bank[:].bitcast(BF16)
+            )
+        qT_view = qT[:].rearrange("p (b g r e) -> p b g r e", b=BATCH, g=WORD_CHUNKS, e=PAIR)
+
+        def key_unit(rows_sb):
+            words = rows_sb[:].bitcast(F32).rearrange("p (j w) -> p j w", j=KEY_TILES)
+            kT = rotating.tile([P, WORD_CHUNKS * PAIR * BANK], BF16, tag="kT")
+
+            def transposes(bank, g, quarters):
+                for j in quarters:
+                    transpose_words(bank[:, j * P : (j + 1) * P], words[:, j, g * P : (g + 1) * P])
+
+            def empty(bank, g):
+                piece = kT[:, g * PAIR * BANK : (g + 1) * PAIR * BANK]
+                if g < SHARED_VECTOR_BANKS:
+                    nc.vector.tensor_copy(out=piece, in_=bank[:].bitcast(BF16))
+                else:
+                    nc.scalar.copy(out=piece, in_=bank[:].bitcast(BF16))
+
+            view = kT[:].rearrange("p (g n e) -> p g n e", g=WORD_CHUNKS, e=PAIR)
+            return {"transposes": transposes, "empty": empty, "view": view}
+
+        def token_unit(rows_sb, vector_banks):
+            words = rows_sb[:].bitcast(F32).rearrange("p (j w) -> p j w", j=KEY_TILES)
+            grouped = rotating.tile([P, PASSES * KEYS * PACK], BF16, tag="x_grouped", align_bytes=64)
+            grouped_words = grouped[:].bitcast(F32).rearrange("p (g n u) -> p g n u", g=PASSES, u=2)
+            codes = rotating.tile([P, PASSES * KEYS], U32, tag="x_codes", align_bytes=64)
+            scales = rotating.tile([P, PASSES * KEYS], U8, tag="x_scales", align_bytes=64)
+
+            def transposes(bank, n, quarters):
+                g, half = divmod(n, 2)
+                for i in quarters:
+                    u, tile_in_half = divmod(i, 2)
+                    transpose_words(
+                        bank[:, i * P : (i + 1) * P],
+                        words[:, 2 * half + tile_in_half, 2 * P * g + u : 2 * P * (g + 1) : 2],
+                    )
+
+            def empty(bank, n):
+                g, half = divmod(n, 2)
+                piece = grouped_words[:, g, half * 2 * P : (half + 1) * 2 * P, :]
+                planes = bank[:].rearrange("p (u n) -> p n u", u=2)
+                if n < vector_banks:
+                    nc.vector.tensor_copy(out=piece, in_=planes)
+                else:
+                    nc.scalar.copy(out=piece, in_=planes)
+
+            def quantise():
+                for g in range(PASSES):
+                    nc.vector.quantize_mx(
+                        out=codes[:, g * KEYS : (g + 1) * KEYS].bitcast(FP8X4),
+                        scales=scales[:, g * KEYS : (g + 1) * KEYS],
+                        in_=grouped[:, g * KEYS * PACK : (g + 1) * KEYS * PACK],
+                    )
+
+            return {
+                "transposes": transposes,
+                "empty": empty,
+                "quantise": quantise,
+                "codes": codes,
+                "scales": scales,
+            }
+
+        def transpose_all(unit):
+            for n in range(UNIT_BANKS):
+                bank = psum.tile([P, BANK], F32, tag="bank")
+                unit["transposes"](bank, n, range(4))
+                unit["empty"](bank, n)
+
+        def softmax_start(score):
+            top = small.tile([P, 1], F32, tag="top")
+            nc.vector.reduce_max(out=top[:], in_=score[:], axis=AXIS.X)
+            shift = small.tile([P, 1], F32, tag="shift")
+            nc.vector.tensor_scalar_mul(out=shift[:], in0=top[:], scalar1=-SCALE)
+            attn = rotating.tile([P, KEYS], F32, tag="attn", bufs=4)
+            total = small.tile([P, 1], F32, tag="total")
+            nc.scalar.activation(
+                out=attn[:], in_=score[:], func=ACT.Exp, bias=shift[:], scale=SCALE, accum_out=total[:]
+            )
+            return attn, total
+
+        def softmax_finish(attn, total):
+            inverse = small.tile([P, 1], F32, tag="inverse")
+            nc.vector.reciprocal(out=inverse[:], in_=total[:])
+            nc.vector.tensor_scalar_mul(out=attn[:], in0=attn[:], scalar1=inverse[:])
+
+        def cast_votes(aw, awi):
+            not_less = rotating.tile([P, KEYS], BF16, tag="not_less")
+            nc.vector.tensor_tensor(out=not_less[:], in0=aw[:], in1=awi[:], op=ALU.is_ge)
+            not_more = rotating.tile([P, KEYS], BF16, tag="not_more")
+            nc.vector.tensor_tensor(out=not_more[:], in0=aw[:], in1=awi[:], op=ALU.is_le)
+            return not_less, not_more
+
+        def count_votes(b, both_votes):
+            counts = psum.tile([P, KEY_TILES * 2 * COUNT_COLS], F32, tag="bank")
+            for j in range(KEY_TILES):
+                for side, votes in enumerate(both_votes):
+                    first = (2 * j + side) * COUNT_COLS
+                    nc.tensor.matmul(
+                        counts[:, first : first + COUNT_COLS],
+                        lhsT=votes[:, j * P : (j + 1) * P],
+                        rhs=vote_share[:],
+                        start=True,
+                        stop=True,
+                    )
+            factors = resident.tile([P, KEY_TILES * 2], F32, name="factors%d" % b)
+            nc.vector.tensor_copy(
+                out=factors[:], in_=counts[:].rearrange("p (i n) -> p i n", n=COUNT_COLS)[:, :, 0]
+            )
+            return factors
+
+        def project(b, stream, unit, factors, scaled_v, key_tiles):
+            out_view = out[b].rearrange("(p j) d -> p j d", j=KEY_TILES)
+            for j in key_tiles:
+                for h in range(DV_HALVES):
+                    acc = psum.tile([P, BANK], F32, tag="bank")
+                    for g in range(PASSES):
+                        tokens = slice(g * KEYS + j * P, g * KEYS + (j + 1) * P)
+                        cols = slice(g * DV + h * BANK, g * DV + (h + 1) * BANK)
+                        nc.tensor.matmul_mx(
+                            out=acc[:],
+                            lhsT=unit["codes"][:, tokens].bitcast(FP8X4),
+                            lhsT_scale=unit["scales"][:, tokens],
+                            rhs=w_codes[:, cols].bitcast(FP8X4),
+                            rhs_scale=w_scales[:, cols],
+                            start=(g == 0),
+                            stop=(g == PASSES - 1),
+                        )
+                    kept = scaled_v[:, j * DV + h * BANK : j * DV + (h + 1) * BANK]
+                    if stream == 0:
+                        nc.scalar.activation(
+                            out=kept, in_=acc[:], func=ACT.Copy, scale=factors[:, 2 * j : 2 * j + 1]
+                        )
+                    else:
+                        mixed = rotating.tile([P, BANK], F32, tag="mixed", bufs=4)
+                        nc.vector.scalar_tensor_tensor(
+                            out=mixed[:],
+                            in0=acc[:],
+                            scalar=factors[:, 2 * j + 1 : 2 * j + 2],
+                            in1=kept,
+                            op0=ALU.mult,
+                            op1=ALU.add,
+                        )
+                        nc.sync.dma_start(
+                            out=out_view[:, j, h * BANK : (h + 1) * BANK], in_=mixed[:]
+                        )
+
+        following = key_unit(keys_sb[0])
+        transpose_all(following)
+        scores = []
+        softmaxes = []
+        votes_of = []
+        for s in range(len(keys_sb)):
+            current = following
+            if s + 1 < len(keys_sb):
+                following = key_unit(keys_sb[s + 1])
+            else:
+                following = token_unit(tokens_sb[0], SHARED_VECTOR_BANKS)
+            if s >= 1:
+                softmaxes.append(softmax_start(scores[s - 1]))
+            score = psum.tile([P, KEYS], F32, tag="bank")
+            scores.append(score)
+            for g in range(WORD_CHUNKS):
+                bank = psum.tile([P, BANK], F32, tag="bank")
+                for e in range(PAIR):
+                    following["transposes"](bank, g, range(2 * e, 2 * e + 2))
+                    nc.tensor.matmul(
+                        score[:],
+                        lhsT=qT_view[:, s // 2, g, :, e],
+                        rhs=current["view"][:, g, :, e],
+                        start=(g == 0 and e == 0),
+                        stop=(g == WORD_CHUNKS - 1 and e == PAIR - 1),
+                    )
+                following["empty"](bank, g)
+            if s >= 1:
+                softmax_finish(*softmaxes[s - 1])
+            if s == 2:
+                votes_of.append(cast_votes(softmaxes[0][0], softmaxes[1][0]))
+
+        units = [following]
+        units[0]["quantise"]()
+        factors_of = [count_votes(0, votes_of[0])]
+        softmaxes.append(softmax_start(scores[3]))
+        units.append(token_unit(tokens_sb[1], UNIT_BANKS))
+        transpose_all(units[1])
+        softmax_finish(*softmaxes[3])
+        votes_of.append(cast_votes(softmaxes[2][0], softmaxes[3][0]))
+
+        for i in range(len(tokens_sb)):
+            b, stream = divmod(i, 2)
+            if stream == 0:
+                scaled_v = rotating.tile([P, KEY_TILES * DV], F32, tag="scaled_v")
+            project(b, stream, units[i], factors_of[b], scaled_v, range(0, KEY_TILES // 2))
+            if i + 1 < len(tokens_sb):
+                units[i + 1]["quantise"]()
+            project(b, stream, units[i], factors_of[b], scaled_v, range(KEY_TILES // 2, KEY_TILES))
+            if i == 0:
+                factors_of.append(count_votes(1, votes_of[1]))
+            if i + 2 < len(tokens_sb):
+                units.append(token_unit(tokens_sb[i + 2], UNIT_BANKS * (i % 2)))
+                transpose_all(units[i + 2])

@@ -14,20 +14,21 @@ AXIS = mybir.AxisListType
 
 P = 128
 BATCH = 2
+STREAMS = 2
 QUERIES = 128
 KEYS = 512
 C = 1024
 DV = 1024
 KEY_TILES = KEYS // P
+HALF_TILES = KEY_TILES // 2
 PAIR = 2
-WORD_CHUNKS = C // PAIR // P
+WORDS = C // PAIR
+WORD_CHUNKS = WORDS // P
 PACK = 4
 PASSES = C // (P * PACK)
 BANK = 512
 DV_HALVES = DV // BANK
 COUNT_COLS = 32
-UNIT_BANKS = 4
-SHARED_VECTOR_BANKS = 1
 SCALE = C**-0.5
 
 FLOPS = 2 * BATCH * 2 * QUERIES * KEYS * C + 2 * BATCH * 2 * KEYS * C * DV
@@ -39,37 +40,56 @@ def tile_crossattention_for_fusion_temporal_pa_kernel(tc, q, k, ki, xs, xis, Wv,
         resident = ctx.enter_context(tc.tile_pool(name="resident", bufs=1))
         rotating = ctx.enter_context(tc.tile_pool(name="rotating", bufs=2))
         small = ctx.enter_context(tc.tile_pool(name="small", bufs=4))
-        psum = ctx.enter_context(tc.psum_pool(name="psum", bufs=8))
+        score_psum = ctx.enter_context(tc.psum_pool(name="score_psum", bufs=2))
+        psum = ctx.enter_context(tc.psum_pool(name="psum", bufs=6))
         ctx.enter_context(tc.manual_schedule())
 
-        w_raw = resident.tile([P, PASSES * PACK * DV], BF16, name="w_raw")
-        for g in range(PASSES):
-            rows = Wv[g * P * PACK : (g + 1) * P * PACK, :]
-            nc.sync.dma_start(
-                out=w_raw[:, g * PACK * DV : (g + 1) * PACK * DV],
-                in_=rows.rearrange("(p t) d -> p (t d)", t=PACK),
-            )
-
-        q_sb = resident.tile([P, BATCH * C], BF16, name="q_sb")
-        nc.sync.dma_start(
-            out=q_sb[:].rearrange("p (b c) -> p b c", b=BATCH), in_=q.rearrange("b r c -> r b c")
-        )
-
-        def load_rows(name, rows):
-            rows_sb = resident.tile([P, KEY_TILES * C], BF16, name=name)
-            nc.sync.dma_start(out=rows_sb[:], in_=rows.rearrange("(p j) c -> p (j c)", j=KEY_TILES))
-            return rows_sb
-
+        q_sb = [resident.tile([P, C], BF16, name="q_sb%d" % b) for b in range(BATCH)]
         keys_sb = [
-            load_rows("keys_sb%d%d" % (b, stream), rows[b])
-            for b in range(BATCH)
-            for stream, rows in enumerate((k, ki))
+            resident.tile([P, KEY_TILES * C], BF16, name="keys_sb%d" % u)
+            for u in range(BATCH * STREAMS)
         ]
         tokens_sb = [
-            load_rows("tokens_sb%d%d" % (b, stream), rows[b])
-            for b in range(BATCH)
-            for stream, rows in enumerate((xs, xis))
+            resident.tile([P, STREAMS * HALF_TILES * C], BF16, name="tokens_sb%d" % i)
+            for i in range(BATCH * 2)
         ]
+        w_raw = [resident.tile([P, PACK * DV], BF16, name="w_raw%d" % g) for g in range(PASSES)]
+
+        def load_queries(b):
+            nc.sync.dma_start(out=q_sb[b][:], in_=q[b])
+
+        def load_keys(unit, parts):
+            b, stream = divmod(unit, STREAMS)
+            rows = (k, ki)[stream][b].rearrange("(p j) c -> p (j c)", j=KEY_TILES)
+            width = KEY_TILES * C // parts
+            for i in range(parts):
+                cols = slice(i * width, (i + 1) * width)
+                nc.sync.dma_start(out=keys_sb[unit][:, cols], in_=rows[:, cols])
+
+        def load_tokens(i):
+            b, half = divmod(i, 2)
+            width = HALF_TILES * C
+            for stream, x in enumerate((xs, xis)):
+                rows = x[b].rearrange("(p j) c -> p (j c)", j=KEY_TILES)
+                nc.sync.dma_start(
+                    out=tokens_sb[i][:, stream * width : (stream + 1) * width],
+                    in_=rows[:, half * width : (half + 1) * width],
+                )
+
+        def load_weights(g):
+            rows = Wv[g * P * PACK : (g + 1) * P * PACK, :]
+            nc.sync.dma_start(out=w_raw[g][:], in_=rows.rearrange("(p t) d -> p (t d)", t=PACK))
+
+        load_queries(0)
+        load_keys(0, 2)
+        load_keys(1, 1)
+        load_weights(0)
+        load_queries(1)
+        load_keys(2, 1)
+        load_weights(1)
+        load_keys(3, 1)
+        for i in range(BATCH * 2):
+            load_tokens(i)
 
         ident = resident.tile([P, P], F32, name="ident")
         make_identity(nc, ident[:])
@@ -80,104 +100,111 @@ def tile_crossattention_for_fusion_temporal_pa_kernel(tc, q, k, ki, xs, xis, Wv,
         one = small.tile([P, 1], F32, tag="one")
         nc.scalar.activation(out=one[:], in_=zero[:], func=ACT.Exp)
 
-        w_grouped = resident.tile([P, PASSES * DV * PACK], BF16, name="w_grouped", align_bytes=64)
-        w_codes = resident.tile([P, PASSES * DV], U32, name="w_codes", align_bytes=64)
-        w_scales = resident.tile([P, PASSES * DV], U8, name="w_scales", align_bytes=64)
-        raw_view = w_raw[:].rearrange("p (g t d) -> p g t d", g=PASSES, t=PACK)
-        grouped_view = w_grouped[:].rearrange("p (g d t) -> p g d t", g=PASSES, t=PACK)
-        for g in range(PASSES):
-            for h in range(DV_HALVES):
-                cols = slice(h * BANK, (h + 1) * BANK)
-                nc.vector.tensor_copy(
-                    out=grouped_view[:, g, cols, :].rearrange("p (c i) t -> p c t i", i=4),
-                    in_=raw_view[:, g, :, cols].rearrange("p t (c i) -> p c t i", i=4),
-                )
-        for g in range(PASSES):
+        w_grouped = [
+            resident.tile([P, DV * PACK], BF16, name="w_grouped%d" % g, align_bytes=64)
+            for g in range(PASSES)
+        ]
+        w_codes = [
+            resident.tile([P, DV], U32, name="w_codes%d" % g, align_bytes=64) for g in range(PASSES)
+        ]
+        w_scales = [
+            resident.tile([P, DV], U8, name="w_scales%d" % g, align_bytes=64) for g in range(PASSES)
+        ]
+
+        def regroup_weights(g, h):
+            cols = slice(h * BANK, (h + 1) * BANK)
+            nc.vector.tensor_copy(
+                out=w_grouped[g][:].rearrange("p (d t) -> p d t", t=PACK)[:, cols, :].rearrange(
+                    "p (c i) t -> p c t i", i=4
+                ),
+                in_=w_raw[g][:].rearrange("p (t d) -> p t d", t=PACK)[:, :, cols].rearrange(
+                    "p t (c i) -> p c t i", i=4
+                ),
+            )
+
+        def quantise_weights(g):
             nc.vector.quantize_mx(
-                out=w_codes[:, g * DV : (g + 1) * DV].bitcast(FP8X4),
-                scales=w_scales[:, g * DV : (g + 1) * DV],
-                in_=w_grouped[:, g * DV * PACK : (g + 1) * DV * PACK],
+                out=w_codes[g][:].bitcast(FP8X4), scales=w_scales[g][:], in_=w_grouped[g][:]
             )
 
         def transpose_words(bank_cols, words):
             nc.tensor.transpose(bank_cols, words, ident[:])
 
-        qT = resident.tile([P, BATCH * PAIR * BANK], BF16, name="qT")
-        q_words = q_sb[:].bitcast(F32)
-        for b in range(BATCH):
-            q_bank = psum.tile([P, BANK], F32, tag="bank")
+        qT = [resident.tile([P, C], BF16, name="qT%d" % b) for b in range(BATCH)]
+
+        def turn_queries(b):
+            bank = psum.tile([P, BANK], F32, tag="bank")
+            words = q_sb[b][:].bitcast(F32)
             for g in range(WORD_CHUNKS):
-                first = (b * WORD_CHUNKS + g) * P
-                transpose_words(q_bank[:, g * P : (g + 1) * P], q_words[:, first : first + P])
-            nc.scalar.copy(
-                out=qT[:, b * PAIR * BANK : (b + 1) * PAIR * BANK], in_=q_bank[:].bitcast(BF16)
-            )
-        qT_view = qT[:].rearrange("p (b g r e) -> p b g r e", b=BATCH, g=WORD_CHUNKS, e=PAIR)
+                transpose_words(bank[:, g * P : (g + 1) * P], words[:, g * P : (g + 1) * P])
+            nc.scalar.copy(out=qT[b][:].bitcast(F32), in_=bank[:])
 
-        def key_unit(rows_sb):
-            words = rows_sb[:].bitcast(F32).rearrange("p (j w) -> p j w", j=KEY_TILES)
+        def key_pieces(unit, engines):
+            words = keys_sb[unit][:].bitcast(F32).rearrange("p (j w) -> p j w", j=KEY_TILES)
             kT = rotating.tile([P, WORD_CHUNKS * PAIR * BANK], BF16, tag="kT")
+            kT_words = kT[:].bitcast(F32)
 
-            def transposes(bank, g, quarters):
-                for j in quarters:
+            def piece(g):
+                bank = psum.tile([P, BANK], F32, tag="bank")
+
+                def transpose(j):
                     transpose_words(bank[:, j * P : (j + 1) * P], words[:, j, g * P : (g + 1) * P])
 
-            def empty(bank, g):
-                piece = kT[:, g * PAIR * BANK : (g + 1) * PAIR * BANK]
-                if g < SHARED_VECTOR_BANKS:
-                    nc.vector.tensor_copy(out=piece, in_=bank[:].bitcast(BF16))
-                else:
-                    nc.scalar.copy(out=piece, in_=bank[:].bitcast(BF16))
+                def empty():
+                    engines[g](out=kT_words[:, g * BANK : (g + 1) * BANK], in_=bank[:])
+
+                return transpose, empty
 
             view = kT[:].rearrange("p (g n e) -> p g n e", g=WORD_CHUNKS, e=PAIR)
-            return {"transposes": transposes, "empty": empty, "view": view}
+            return piece, view
 
-        def token_unit(rows_sb, vector_banks):
-            words = rows_sb[:].bitcast(F32).rearrange("p (j w) -> p j w", j=KEY_TILES)
-            grouped = rotating.tile([P, PASSES * KEYS * PACK], BF16, tag="x_grouped", align_bytes=64)
-            grouped_words = grouped[:].bitcast(F32).rearrange("p (g n u) -> p g n u", g=PASSES, u=2)
-            codes = rotating.tile([P, PASSES * KEYS], U32, tag="x_codes", align_bytes=64)
-            scales = rotating.tile([P, PASSES * KEYS], U8, tag="x_scales", align_bytes=64)
+        grouped_of = {}
+        quantised_of = {}
 
-            def transposes(bank, n, quarters):
-                g, half = divmod(n, 2)
-                for i in quarters:
-                    u, tile_in_half = divmod(i, 2)
-                    transpose_words(
-                        bank[:, i * P : (i + 1) * P],
-                        words[:, 2 * half + tile_in_half, 2 * P * g + u : 2 * P * (g + 1) : 2],
-                    )
+        def token_piece(step, stream, engine):
+            b, j = divmod(step, KEY_TILES)
+            half, tile_in_half = divmod(j, HALF_TILES)
+            first = (stream * HALF_TILES + tile_in_half) * WORDS
+            words = tokens_sb[2 * b + half][:].bitcast(F32)[:, first : first + WORDS]
+            if stream == 0:
+                grouped = rotating.tile([P, STREAMS * C], BF16, tag="grouped", align_bytes=64, bufs=3)
+                grouped_of[step] = grouped
+            grouped = grouped_of[step]
+            bank = psum.tile([P, BANK], F32, tag="bank")
 
-            def empty(bank, n):
-                g, half = divmod(n, 2)
-                piece = grouped_words[:, g, half * 2 * P : (half + 1) * 2 * P, :]
-                planes = bank[:].rearrange("p (u n) -> p n u", u=2)
-                if n < vector_banks:
-                    nc.vector.tensor_copy(out=piece, in_=planes)
-                else:
-                    nc.scalar.copy(out=piece, in_=planes)
+            def transpose(i):
+                g, u = divmod(i, 2)
+                transpose_words(
+                    bank[:, i * P : (i + 1) * P], words[:, 2 * P * g + u : 2 * P * (g + 1) : 2]
+                )
 
-            def quantise():
-                for g in range(PASSES):
-                    nc.vector.quantize_mx(
-                        out=codes[:, g * KEYS : (g + 1) * KEYS].bitcast(FP8X4),
-                        scales=scales[:, g * KEYS : (g + 1) * KEYS],
-                        in_=grouped[:, g * KEYS * PACK : (g + 1) * KEYS * PACK],
-                    )
+            def empty():
+                engine(
+                    out=grouped[:].bitcast(F32)[:, stream * WORDS : (stream + 1) * WORDS].rearrange(
+                        "p (g n u) -> p g n u", g=PASSES, u=2
+                    ),
+                    in_=bank[:].rearrange("p (g u n) -> p g n u", g=PASSES, u=2),
+                )
 
-            return {
-                "transposes": transposes,
-                "empty": empty,
-                "quantise": quantise,
-                "codes": codes,
-                "scales": scales,
-            }
+            return transpose, empty
 
-        def transpose_all(unit):
-            for n in range(UNIT_BANKS):
-                bank = psum.tile([P, BANK], F32, tag="bank")
-                unit["transposes"](bank, n, range(4))
-                unit["empty"](bank, n)
+        def run_piece(piece):
+            transpose, empty = piece
+            for i in range(4):
+                transpose(i)
+            empty()
+
+        def turn_tokens(step):
+            run_piece(token_piece(step, 0, nc.scalar.copy))
+            run_piece(token_piece(step, 1, nc.vector.tensor_copy))
+
+        def quantise_tokens(step):
+            codes = rotating.tile([P, STREAMS * PASSES * P], U32, tag="codes", align_bytes=64, bufs=3)
+            scales = rotating.tile([P, STREAMS * PASSES * P], U8, tag="scales", align_bytes=64, bufs=3)
+            nc.vector.quantize_mx(
+                out=codes[:].bitcast(FP8X4), scales=scales[:], in_=grouped_of[step][:]
+            )
+            quantised_of[step] = (codes, scales)
 
         def softmax_start(score):
             top = small.tile([P, 1], F32, tag="top")
@@ -204,7 +231,7 @@ def tile_crossattention_for_fusion_temporal_pa_kernel(tc, q, k, ki, xs, xis, Wv,
             return not_less, not_more
 
         def count_votes(b, both_votes):
-            counts = psum.tile([P, KEY_TILES * 2 * COUNT_COLS], F32, tag="bank")
+            counts = score_psum.tile([P, KEY_TILES * 2 * COUNT_COLS], F32, tag="score")
             for j in range(KEY_TILES):
                 for side, votes in enumerate(both_votes):
                     first = (2 * j + side) * COUNT_COLS
@@ -221,93 +248,105 @@ def tile_crossattention_for_fusion_temporal_pa_kernel(tc, q, k, ki, xs, xis, Wv,
             )
             return factors
 
-        def project(b, stream, unit, factors, scaled_v, key_tiles):
-            out_view = out[b].rearrange("(p j) d -> p j d", j=KEY_TILES)
-            for j in key_tiles:
+        def project(step, factors):
+            b, j = divmod(step, KEY_TILES)
+            codes, scales = quantised_of[step]
+            kept = rotating.tile([P, DV], F32, tag="kept", bufs=3)
+            mixed = rotating.tile([P, DV], F32, tag="mixed", bufs=4)
+            out_rows = out[b].rearrange("(p j) d -> p j d", j=KEY_TILES)[:, j, :]
+            for stream in range(STREAMS):
                 for h in range(DV_HALVES):
+                    cols = slice(h * BANK, (h + 1) * BANK)
                     acc = psum.tile([P, BANK], F32, tag="bank")
                     for g in range(PASSES):
-                        tokens = slice(g * KEYS + j * P, g * KEYS + (j + 1) * P)
-                        cols = slice(g * DV + h * BANK, g * DV + (h + 1) * BANK)
+                        first = (stream * PASSES + g) * P
                         nc.tensor.matmul_mx(
                             out=acc[:],
-                            lhsT=unit["codes"][:, tokens].bitcast(FP8X4),
-                            lhsT_scale=unit["scales"][:, tokens],
-                            rhs=w_codes[:, cols].bitcast(FP8X4),
-                            rhs_scale=w_scales[:, cols],
+                            lhsT=codes[:, first : first + P].bitcast(FP8X4),
+                            lhsT_scale=scales[:, first : first + P],
+                            rhs=w_codes[g][:, cols].bitcast(FP8X4),
+                            rhs_scale=w_scales[g][:, cols],
                             start=(g == 0),
                             stop=(g == PASSES - 1),
                         )
-                    kept = scaled_v[:, j * DV + h * BANK : j * DV + (h + 1) * BANK]
                     if stream == 0:
                         nc.scalar.activation(
-                            out=kept, in_=acc[:], func=ACT.Copy, scale=factors[:, 2 * j : 2 * j + 1]
+                            out=kept[:, cols], in_=acc[:], func=ACT.Copy, scale=factors[:, 2 * j : 2 * j + 1]
                         )
                     else:
-                        mixed = rotating.tile([P, BANK], F32, tag="mixed", bufs=4)
                         nc.vector.scalar_tensor_tensor(
-                            out=mixed[:],
+                            out=mixed[:, cols],
                             in0=acc[:],
                             scalar=factors[:, 2 * j + 1 : 2 * j + 2],
-                            in1=kept,
+                            in1=kept[:, cols],
                             op0=ALU.mult,
                             op1=ALU.add,
                         )
-                        nc.sync.dma_start(
-                            out=out_view[:, j, h * BANK : (h + 1) * BANK], in_=mixed[:]
-                        )
+                        nc.sync.dma_start(out=out_rows[:, cols], in_=mixed[:, cols])
 
-        following = key_unit(keys_sb[0])
-        transpose_all(following)
+        on_scalar, on_vector = nc.scalar.copy, nc.vector.tensor_copy
+        turn_queries(0)
+        piece, current = key_pieces(0, (on_vector, on_scalar, on_vector, on_scalar))
+        for g in range(WORD_CHUNKS):
+            run_piece(piece(g))
         scores = []
         softmaxes = []
         votes_of = []
-        for s in range(len(keys_sb)):
-            current = following
-            if s + 1 < len(keys_sb):
-                following = key_unit(keys_sb[s + 1])
+        units = BATCH * STREAMS
+        for s in range(units):
+            if s == 1:
+                turn_queries(1)
+            if s + 1 < units:
+                piece, following = key_pieces(s + 1, (on_scalar, on_scalar, on_scalar, on_scalar))
+                pieces = [lambda g=g: piece(g) for g in range(WORD_CHUNKS)]
             else:
-                following = token_unit(tokens_sb[0], SHARED_VECTOR_BANKS)
+                following = None
+                pieces = [
+                    lambda step=step, stream=stream: token_piece(step, stream, on_scalar)
+                    for step in range(2)
+                    for stream in range(STREAMS)
+                ]
+            if 1 <= s <= PASSES:
+                for h in range(DV_HALVES):
+                    regroup_weights(s - 1, h)
             if s >= 1:
                 softmaxes.append(softmax_start(scores[s - 1]))
-            score = psum.tile([P, KEYS], F32, tag="bank")
+            if 1 <= s <= PASSES:
+                quantise_weights(s - 1)
+            score = score_psum.tile([P, KEYS], F32, tag="score")
             scores.append(score)
             for g in range(WORD_CHUNKS):
-                bank = psum.tile([P, BANK], F32, tag="bank")
+                transpose, empty = pieces[g]()
                 for e in range(PAIR):
-                    following["transposes"](bank, g, range(2 * e, 2 * e + 2))
+                    transpose(2 * e)
+                    transpose(2 * e + 1)
                     nc.tensor.matmul(
                         score[:],
-                        lhsT=qT_view[:, s // 2, g, :, e],
-                        rhs=current["view"][:, g, :, e],
+                        lhsT=qT[s // STREAMS][:].rearrange("p (g r e) -> p g r e", g=WORD_CHUNKS, e=PAIR)[
+                            :, g, :, e
+                        ],
+                        rhs=current[:, g, :, e],
                         start=(g == 0 and e == 0),
                         stop=(g == WORD_CHUNKS - 1 and e == PAIR - 1),
                     )
-                following["empty"](bank, g)
+                empty()
+            current = following
             if s >= 1:
                 softmax_finish(*softmaxes[s - 1])
             if s == 2:
                 votes_of.append(cast_votes(softmaxes[0][0], softmaxes[1][0]))
-
-        units = [following]
-        units[0]["quantise"]()
         factors_of = [count_votes(0, votes_of[0])]
         softmaxes.append(softmax_start(scores[3]))
-        units.append(token_unit(tokens_sb[1], UNIT_BANKS))
-        transpose_all(units[1])
+        quantise_tokens(0)
         softmax_finish(*softmaxes[3])
         votes_of.append(cast_votes(softmaxes[2][0], softmaxes[3][0]))
 
-        for i in range(len(tokens_sb)):
-            b, stream = divmod(i, 2)
-            if stream == 0:
-                scaled_v = rotating.tile([P, KEY_TILES * DV], F32, tag="scaled_v")
-            project(b, stream, units[i], factors_of[b], scaled_v, range(0, KEY_TILES // 2))
-            if i + 1 < len(tokens_sb):
-                units[i + 1]["quantise"]()
-            project(b, stream, units[i], factors_of[b], scaled_v, range(KEY_TILES // 2, KEY_TILES))
-            if i == 0:
+        steps = BATCH * KEY_TILES
+        for step in range(steps):
+            if step + 2 < steps:
+                turn_tokens(step + 2)
+            if step == 1:
                 factors_of.append(count_votes(1, votes_of[1]))
-            if i + 2 < len(tokens_sb):
-                units.append(token_unit(tokens_sb[i + 2], UNIT_BANKS * (i % 2)))
-                transpose_all(units[i + 2])
+            if step + 1 < steps:
+                quantise_tokens(step + 1)
+            project(step, factors_of[step // KEY_TILES])

@@ -158,6 +158,20 @@ def tile_crossattention_for_fusion_temporal_pa_kernel(tc, q, k, ki, xs, xis, Wv,
             view = kT[:].rearrange("p (g n e) -> p g n e", g=WORD_CHUNKS, e=PAIR)
             return piece, view
 
+        SPLIT0 = 2
+        split_of = [
+            resident.tile([P, STREAMS * HALF_TILES * C], BF16, name="split%d" % i)
+            for i in range(BATCH * 2)
+        ]
+
+        def split_words(i, stream, engine):
+            width = HALF_TILES * WORDS
+            cols = slice(stream * width, (stream + 1) * width)
+            engine(
+                out=split_of[i][:].bitcast(F32)[:, cols].rearrange("p (j u w) -> p j u w", j=HALF_TILES, u=2),
+                in_=tokens_sb[i][:].bitcast(F32)[:, cols].rearrange("p (j w u) -> p j u w", j=HALF_TILES, u=2),
+            )
+
         grouped_of = {}
         quantised_of = {}
 
@@ -165,9 +179,9 @@ def tile_crossattention_for_fusion_temporal_pa_kernel(tc, q, k, ki, xs, xis, Wv,
             b, j = divmod(step, KEY_TILES)
             half, tile_in_half = divmod(j, HALF_TILES)
             first = (stream * HALF_TILES + tile_in_half) * WORDS
-            words = tokens_sb[2 * b + half][:].bitcast(F32)[:, first : first + WORDS]
+            words = (tokens_sb if step<SPLIT0 else split_of)[2 * b + half][:].bitcast(F32)[:, first : first + WORDS]
             if stream == 0:
-                grouped = rotating.tile([P, STREAMS * C], BF16, tag="grouped", align_bytes=64, bufs=3)
+                grouped = rotating.tile([P, STREAMS * C], BF16, tag="grouped", align_bytes=64, bufs=4)
                 grouped_of[step] = grouped
             grouped = grouped_of[step]
             bank = psum.tile([P, BANK], F32, tag="bank")
@@ -175,7 +189,7 @@ def tile_crossattention_for_fusion_temporal_pa_kernel(tc, q, k, ki, xs, xis, Wv,
             def transpose(i):
                 g, u = divmod(i, 2)
                 transpose_words(
-                    bank[:, i * P : (i + 1) * P], words[:, 2 * P * g + u : 2 * P * (g + 1) : 2]
+                    bank[:, i * P : (i + 1) * P], (words[:, 2 * P * g + u : 2 * P * (g + 1) : 2] if step<SPLIT0 else words[:, u * 2 * P + g * P : u * 2 * P + (g + 1) * P])
                 )
 
             def empty():
@@ -199,8 +213,8 @@ def tile_crossattention_for_fusion_temporal_pa_kernel(tc, q, k, ki, xs, xis, Wv,
             run_piece(token_piece(step, 1, nc.vector.tensor_copy))
 
         def quantise_tokens(step):
-            codes = rotating.tile([P, STREAMS * PASSES * P], U32, tag="codes", align_bytes=64, bufs=3)
-            scales = rotating.tile([P, STREAMS * PASSES * P], U8, tag="scales", align_bytes=64, bufs=3)
+            codes = rotating.tile([P, STREAMS * PASSES * P], U32, tag="codes", align_bytes=64, bufs=4)
+            scales = rotating.tile([P, STREAMS * PASSES * P], U8, tag="scales", align_bytes=64, bufs=4)
             nc.vector.quantize_mx(
                 out=codes[:].bitcast(FP8X4), scales=scales[:], in_=grouped_of[step][:]
             )
@@ -335,18 +349,33 @@ def tile_crossattention_for_fusion_temporal_pa_kernel(tc, q, k, ki, xs, xis, Wv,
                 softmax_finish(*softmaxes[s - 1])
             if s == 2:
                 votes_of.append(cast_votes(softmaxes[0][0], softmaxes[1][0]))
-        factors_of = [count_votes(0, votes_of[0])]
-        softmaxes.append(softmax_start(scores[3]))
         quantise_tokens(0)
-        softmax_finish(*softmaxes[3])
-        votes_of.append(cast_votes(softmaxes[2][0], softmaxes[3][0]))
+        factors_of = [count_votes(0, votes_of[0])]
+        quantise_tokens(1)
+        split_words(1, 1, nc.gpsimd.tensor_copy)
+        split_words(1, 0, nc.gpsimd.tensor_copy)
 
-        steps = BATCH * KEY_TILES
-        for step in range(steps):
-            if step + 2 < steps:
-                turn_tokens(step + 2)
-            if step == 1:
+        rounds = BATCH * KEY_TILES // HALF_TILES
+        for i in range(rounds):
+            first, second = HALF_TILES * i, HALF_TILES * i + 1
+            factors = factors_of[i // 2]
+            project(first, factors)
+            if i == 0:
+                softmaxes.append(softmax_start(scores[3]))
+            if i + 1 < rounds:
+                turn_tokens(first + HALF_TILES)
+                turn_tokens(second + HALF_TILES)
+            if i == 1:
                 factors_of.append(count_votes(1, votes_of[1]))
-            if step + 1 < steps:
-                quantise_tokens(step + 1)
-            project(step, factors_of[step // KEY_TILES])
+            if i + 1 < rounds:
+                quantise_tokens(first + HALF_TILES)
+            if i == 0:
+                softmax_finish(*softmaxes[3])
+            project(second, factors)
+            if i == 0:
+                votes_of.append(cast_votes(softmaxes[2][0], softmaxes[3][0]))
+            if i + 1 < rounds:
+                quantise_tokens(second + HALF_TILES)
+            if i + 2 < rounds:
+                split_words(i + 2, 1, nc.gpsimd.tensor_copy)
+                split_words(i + 2, 0, nc.gpsimd.tensor_copy)

@@ -50,8 +50,8 @@ def tile_crossattention_for_fusion_temporal_pa_kernel(tc, q, k, ki, xs, xis, Wv,
             for u in range(BATCH * STREAMS)
         ]
         tokens_sb = [
-            resident.tile([P, STREAMS * HALF_TILES * C], BF16, name="tokens_sb%d" % i)
-            for i in range(BATCH * 2)
+            resident.tile([P, STREAMS * C], BF16, name="tokens_sb%d" % step)
+            for step in range(BATCH * KEY_TILES)
         ]
         w_raw = [resident.tile([P, PACK * DV], BF16, name="w_raw%d" % g) for g in range(PASSES)]
 
@@ -66,14 +66,12 @@ def tile_crossattention_for_fusion_temporal_pa_kernel(tc, q, k, ki, xs, xis, Wv,
                 cols = slice(i * width, (i + 1) * width)
                 nc.sync.dma_start(out=keys_sb[unit][:, cols], in_=rows[:, cols])
 
-        def load_tokens(i):
-            b, half = divmod(i, 2)
-            width = HALF_TILES * C
+        def load_tokens(step):
+            b, j = divmod(step, KEY_TILES)
             for stream, x in enumerate((xs, xis)):
-                rows = x[b].rearrange("(p j) c -> p (j c)", j=KEY_TILES)
                 nc.sync.dma_start(
-                    out=tokens_sb[i][:, stream * width : (stream + 1) * width],
-                    in_=rows[:, half * width : (half + 1) * width],
+                    out=tokens_sb[step][:, stream * C : (stream + 1) * C],
+                    in_=x[b].rearrange("(p j) c -> p j c", j=KEY_TILES)[:, j, :],
                 )
 
         def load_weights(g):
@@ -83,13 +81,13 @@ def tile_crossattention_for_fusion_temporal_pa_kernel(tc, q, k, ki, xs, xis, Wv,
         load_queries(0)
         load_keys(0, 2)
         load_keys(1, 1)
-        load_weights(0)
         load_queries(1)
         load_keys(2, 1)
-        load_weights(1)
         load_keys(3, 1)
-        for i in range(BATCH * 2):
-            load_tokens(i)
+        load_weights(0)
+        load_weights(1)
+        for step in range(BATCH * KEY_TILES):
+            load_tokens(step)
 
         ident = resident.tile([P, P], F32, name="ident")
         make_identity(nc, ident[:])
@@ -111,9 +109,9 @@ def tile_crossattention_for_fusion_temporal_pa_kernel(tc, q, k, ki, xs, xis, Wv,
             resident.tile([P, DV], U8, name="w_scales%d" % g, align_bytes=64) for g in range(PASSES)
         ]
 
-        def regroup_weights(g, h):
+        def regroup_weights(g, h, engine):
             cols = slice(h * BANK, (h + 1) * BANK)
-            nc.vector.tensor_copy(
+            engine.tensor_copy(
                 out=w_grouped[g][:].rearrange("p (d t) -> p d t", t=PACK)[:, cols, :].rearrange(
                     "p (c i) t -> p c t i", i=4
                 ),
@@ -122,9 +120,12 @@ def tile_crossattention_for_fusion_temporal_pa_kernel(tc, q, k, ki, xs, xis, Wv,
                 ),
             )
 
-        def quantise_weights(g):
+        def quantise_weights(g, h):
+            cols = slice(h * BANK, (h + 1) * BANK)
             nc.vector.quantize_mx(
-                out=w_codes[g][:].bitcast(FP8X4), scales=w_scales[g][:], in_=w_grouped[g][:]
+                out=w_codes[g][:, cols].bitcast(FP8X4),
+                scales=w_scales[g][:, cols],
+                in_=w_grouped[g][:, h * BANK * PACK : (h + 1) * BANK * PACK],
             )
 
         def transpose_words(bank_cols, words):
@@ -158,28 +159,24 @@ def tile_crossattention_for_fusion_temporal_pa_kernel(tc, q, k, ki, xs, xis, Wv,
             view = kT[:].rearrange("p (g n e) -> p g n e", g=WORD_CHUNKS, e=PAIR)
             return piece, view
 
-        SPLIT0 = 2
-        split_of = [
-            resident.tile([P, STREAMS * HALF_TILES * C], BF16, name="split%d" % i)
-            for i in range(BATCH * 2)
-        ]
+        SPLIT = (2, 3, 4, 5, 6, 7)
+        split_of = {}
 
-        def split_words(i, stream, engine):
-            width = HALF_TILES * WORDS
-            cols = slice(stream * width, (stream + 1) * width)
+        def split_words(step, engine):
+            split = rotating.tile([P, STREAMS * C], BF16, tag="split", bufs=4)
+            split_of[step] = split
             engine(
-                out=split_of[i][:].bitcast(F32)[:, cols].rearrange("p (j u w) -> p j u w", j=HALF_TILES, u=2),
-                in_=tokens_sb[i][:].bitcast(F32)[:, cols].rearrange("p (j w u) -> p j u w", j=HALF_TILES, u=2),
+                out=split[:].bitcast(F32).rearrange("p (n u w) -> p n u w", n=STREAMS, u=2),
+                in_=tokens_sb[step][:].bitcast(F32).rearrange("p (n w u) -> p n u w", n=STREAMS, u=2),
             )
 
         grouped_of = {}
         quantised_of = {}
 
         def token_piece(step, stream, engine):
-            b, j = divmod(step, KEY_TILES)
-            half, tile_in_half = divmod(j, HALF_TILES)
-            first = (stream * HALF_TILES + tile_in_half) * WORDS
-            words = (tokens_sb if step<SPLIT0 else split_of)[2 * b + half][:].bitcast(F32)[:, first : first + WORDS]
+            words = (split_of if step in SPLIT else tokens_sb)[step][:].bitcast(F32)[
+                :, stream * WORDS : (stream + 1) * WORDS
+            ]
             if stream == 0:
                 grouped = rotating.tile([P, STREAMS * C], BF16, tag="grouped", align_bytes=64, bufs=4)
                 grouped_of[step] = grouped
@@ -189,7 +186,7 @@ def tile_crossattention_for_fusion_temporal_pa_kernel(tc, q, k, ki, xs, xis, Wv,
             def transpose(i):
                 g, u = divmod(i, 2)
                 transpose_words(
-                    bank[:, i * P : (i + 1) * P], (words[:, 2 * P * g + u : 2 * P * (g + 1) : 2] if step<SPLIT0 else words[:, u * 2 * P + g * P : u * 2 * P + (g + 1) * P])
+                    bank[:, i * P : (i + 1) * P], (words[:, 2 * P * g + u : 2 * P * (g + 1) : 2] if step not in SPLIT else words[:, u * 2 * P + g * P : u * 2 * P + (g + 1) * P])
                 )
 
             def empty():
@@ -262,14 +259,16 @@ def tile_crossattention_for_fusion_temporal_pa_kernel(tc, q, k, ki, xs, xis, Wv,
             )
             return factors
 
-        def project(step, factors):
+        def project(step, factors, last=False):
             b, j = divmod(step, KEY_TILES)
             codes, scales = quantised_of[step]
             kept = rotating.tile([P, DV], F32, tag="kept", bufs=3)
             mixed = rotating.tile([P, DV], F32, tag="mixed", bufs=4)
             out_rows = out[b].rearrange("(p j) d -> p j d", j=KEY_TILES)[:, j, :]
-            for stream in range(STREAMS):
-                for h in range(DV_HALVES):
+            pairs = [(stream, h) for stream in range(STREAMS) for h in range(DV_HALVES)]
+            if last:
+                pairs = [(stream, h) for h in range(DV_HALVES) for stream in range(STREAMS)]
+            for stream, h in pairs:
                     cols = slice(h * BANK, (h + 1) * BANK)
                     acc = psum.tile([P, BANK], F32, tag="bank")
                     for g in range(PASSES):
@@ -299,83 +298,87 @@ def tile_crossattention_for_fusion_temporal_pa_kernel(tc, q, k, ki, xs, xis, Wv,
                         nc.sync.dma_start(out=out_rows[:, cols], in_=mixed[:, cols])
 
         on_scalar, on_vector = nc.scalar.copy, nc.vector.tensor_copy
-        turn_queries(0)
-        piece, current = key_pieces(0, (on_vector, on_scalar, on_vector, on_scalar))
-        for g in range(WORD_CHUNKS):
-            run_piece(piece(g))
-        scores = []
-        softmaxes = []
-        votes_of = []
-        units = BATCH * STREAMS
-        for s in range(units):
-            if s == 1:
-                turn_queries(1)
-            if s + 1 < units:
-                piece, following = key_pieces(s + 1, (on_scalar, on_scalar, on_scalar, on_scalar))
-                pieces = [lambda g=g: piece(g) for g in range(WORD_CHUNKS)]
-            else:
-                following = None
-                pieces = [
-                    lambda step=step, stream=stream: token_piece(step, stream, on_scalar)
-                    for step in range(2)
-                    for stream in range(STREAMS)
-                ]
-            if 1 <= s <= PASSES:
-                for h in range(DV_HALVES):
-                    regroup_weights(s - 1, h)
-            if s >= 1:
-                softmaxes.append(softmax_start(scores[s - 1]))
-            if 1 <= s <= PASSES:
-                quantise_weights(s - 1)
+        scores = {}
+        softmaxes = {}
+        votes_of = {}
+        factors_of = {}
+
+        def score_unit(unit, view, pieces):
             score = score_psum.tile([P, KEYS], F32, tag="score")
-            scores.append(score)
+            scores[unit] = score
             for g in range(WORD_CHUNKS):
-                transpose, empty = pieces[g]()
+                if pieces:
+                    transpose, empty = pieces[g]()
                 for e in range(PAIR):
-                    transpose(2 * e)
-                    transpose(2 * e + 1)
+                    if pieces:
+                        transpose(2 * e)
+                        transpose(2 * e + 1)
                     nc.tensor.matmul(
                         score[:],
-                        lhsT=qT[s // STREAMS][:].rearrange("p (g r e) -> p g r e", g=WORD_CHUNKS, e=PAIR)[
+                        lhsT=qT[unit // STREAMS][:].rearrange("p (g r e) -> p g r e", g=WORD_CHUNKS, e=PAIR)[
                             :, g, :, e
                         ],
-                        rhs=current[:, g, :, e],
+                        rhs=view[:, g, :, e],
                         start=(g == 0 and e == 0),
                         stop=(g == WORD_CHUNKS - 1 and e == PAIR - 1),
                     )
-                empty()
-            current = following
-            if s >= 1:
-                softmax_finish(*softmaxes[s - 1])
-            if s == 2:
-                votes_of.append(cast_votes(softmaxes[0][0], softmaxes[1][0]))
-        quantise_tokens(0)
-        factors_of = [count_votes(0, votes_of[0])]
-        quantise_tokens(1)
-        split_words(1, 1, nc.gpsimd.tensor_copy)
-        split_words(1, 0, nc.gpsimd.tensor_copy)
+                if pieces:
+                    empty()
 
-        rounds = BATCH * KEY_TILES // HALF_TILES
-        for i in range(rounds):
-            first, second = HALF_TILES * i, HALF_TILES * i + 1
-            factors = factors_of[i // 2]
-            project(first, factors)
-            if i == 0:
-                softmaxes.append(softmax_start(scores[3]))
-            if i + 1 < rounds:
-                turn_tokens(first + HALF_TILES)
-                turn_tokens(second + HALF_TILES)
-            if i == 1:
-                factors_of.append(count_votes(1, votes_of[1]))
-            if i + 1 < rounds:
-                quantise_tokens(first + HALF_TILES)
-            if i == 0:
-                softmax_finish(*softmaxes[3])
-            project(second, factors)
-            if i == 0:
-                votes_of.append(cast_votes(softmaxes[2][0], softmaxes[3][0]))
-            if i + 1 < rounds:
-                quantise_tokens(second + HALF_TILES)
-            if i + 2 < rounds:
-                split_words(i + 2, 1, nc.gpsimd.tensor_copy)
-                split_words(i + 2, 0, nc.gpsimd.tensor_copy)
+        def bound(make, *args):
+            return lambda: make(*args)
+
+        turn_queries(0)
+        piece, view0 = key_pieces(0, (on_vector, on_scalar, on_vector, on_scalar))
+        for g in range(WORD_CHUNKS):
+            run_piece(piece(g))
+        piece, view1 = key_pieces(1, (on_scalar, on_scalar, on_scalar, on_scalar))
+        score_unit(0, view0, [bound(piece, g) for g in range(WORD_CHUNKS)])
+        turn_queries(1)
+        softmaxes[0] = softmax_start(scores[0])
+        piece, view2 = key_pieces(2, (on_scalar, on_scalar, on_scalar, on_scalar))
+        score_unit(1, view1, [bound(piece, g) for g in range(WORD_CHUNKS)])
+        softmax_finish(*softmaxes[0])
+        softmaxes[1] = softmax_start(scores[1])
+        piece, view3 = key_pieces(3, (on_scalar, on_scalar, on_scalar, on_scalar))
+        score_unit(2, view2, [bound(piece, g) for g in range(WORD_CHUNKS)])
+        regroup_weights(0, 0, nc.vector)
+        regroup_weights(0, 1, nc.gpsimd)
+        softmax_finish(*softmaxes[1])
+        quantise_weights(0, 0)
+        softmaxes[2] = softmax_start(scores[2])
+        score_unit(3, view3, None)
+        regroup_weights(1, 0, nc.vector)
+        regroup_weights(1, 1, nc.gpsimd)
+        quantise_weights(0, 1)
+        votes_of[0] = cast_votes(softmaxes[0][0], softmaxes[1][0])
+        quantise_weights(1, 0)
+        softmax_finish(*softmaxes[2])
+        run_piece(token_piece(0, 0, on_scalar))
+        run_piece(token_piece(0, 1, on_scalar))
+        factors_of[0] = count_votes(0, votes_of[0])
+        run_piece(token_piece(1, 0, on_scalar))
+        run_piece(token_piece(1, 1, on_scalar))
+        quantise_tokens(0)
+        quantise_weights(1, 1)
+        softmaxes[3] = softmax_start(scores[3])
+        quantise_tokens(1)
+        for step in (2, 3):
+            split_words(step, nc.gpsimd.tensor_copy)
+        project(0, factors_of[0])
+        softmax_finish(*softmaxes[3])
+        for step in (2, 4, 6):
+            turn_tokens(step)
+            turn_tokens(step + 1)
+            quantise_tokens(step)
+            if step == 2:
+                votes_of[1] = cast_votes(softmaxes[2][0], softmaxes[3][0])
+            if step == 4:
+                factors_of[1] = count_votes(1, votes_of[1])
+            project(step - 1, factors_of[(step - 1) // KEY_TILES])
+            quantise_tokens(step + 1)
+            for later in (step + 2, step + 3):
+                if later < 8:
+                    split_words(later, nc.gpsimd.tensor_copy)
+            project(step, factors_of[step // KEY_TILES])
+        project(7, factors_of[1], True)

@@ -111,14 +111,15 @@ def tile_crossattention_for_fusion_temporal_pa_kernel(tc, q, k, ki, xs, xis, Wv,
 
         def regroup_weights(g, h, engine):
             cols = slice(h * BANK, (h + 1) * BANK)
-            engine.tensor_copy(
-                out=w_grouped[g][:].rearrange("p (d t) -> p d t", t=PACK)[:, cols, :].rearrange(
-                    "p (c i) t -> p c t i", i=4
-                ),
-                in_=w_raw[g][:].rearrange("p (t d) -> p t d", t=PACK)[:, :, cols].rearrange(
-                    "p t (c i) -> p c t i", i=4
-                ),
-            )
+            grouped = w_grouped[g][:].rearrange("p (d t) -> p d t", t=PACK)[:, cols, :]
+            raw = w_raw[g][:].rearrange("p (t d) -> p t d", t=PACK)[:, :, cols]
+            if engine is nc.gpsimd:
+                engine.tensor_copy(out=grouped, in_=raw.rearrange("p t d -> p d t"))
+            else:
+                engine.tensor_copy(
+                    out=grouped.rearrange("p (c i) t -> p c t i", i=4),
+                    in_=raw.rearrange("p t (c i) -> p c t i", i=4),
+                )
 
         def quantise_weights(g, h):
             cols = slice(h * BANK, (h + 1) * BANK)

@@ -83,8 +83,8 @@ def tile_crossattention_for_fusion_temporal_pa_kernel(tc, q, k, ki, xs, xis, Wv,
         load_keys(1, 1)
         load_queries(1)
         load_keys(2, 1)
-        load_keys(3, 1)
         load_weights(0)
+        load_keys(3, 1)
         load_weights(1)
         for step in range(BATCH * KEY_TILES):
             load_tokens(step)
@@ -116,7 +116,7 @@ def tile_crossattention_for_fusion_temporal_pa_kernel(tc, q, k, ki, xs, xis, Wv,
             if engine is nc.gpsimd:
                 engine.tensor_copy(out=grouped, in_=raw.rearrange("p t d -> p d t"))
             else:
-                engine.tensor_copy(
+                (engine.copy if engine is nc.scalar else engine.tensor_copy)(
                     out=grouped.rearrange("p (c i) t -> p c t i", i=4),
                     in_=raw.rearrange("p t (c i) -> p c t i", i=4),
                 )
@@ -160,7 +160,7 @@ def tile_crossattention_for_fusion_temporal_pa_kernel(tc, q, k, ki, xs, xis, Wv,
             view = kT[:].rearrange("p (g n e) -> p g n e", g=WORD_CHUNKS, e=PAIR)
             return piece, view
 
-        SPLIT = (2, 3, 4, 5, 6, 7)
+        SPLIT = ()
         split_of = {}
 
         def split_words(step, engine):
@@ -208,7 +208,7 @@ def tile_crossattention_for_fusion_temporal_pa_kernel(tc, q, k, ki, xs, xis, Wv,
 
         def turn_tokens(step):
             run_piece(token_piece(step, 0, nc.scalar.copy))
-            run_piece(token_piece(step, 1, nc.vector.tensor_copy))
+            run_piece(token_piece(step, 1, nc.scalar.copy))
 
         def quantise_tokens(step):
             codes = rotating.tile([P, STREAMS * PASSES * P], U32, tag="codes", align_bytes=64, bufs=4)
@@ -243,7 +243,7 @@ def tile_crossattention_for_fusion_temporal_pa_kernel(tc, q, k, ki, xs, xis, Wv,
             return not_less, not_more
 
         def count_votes(b, both_votes):
-            counts = score_psum.tile([P, KEY_TILES * 2 * COUNT_COLS], F32, tag="score")
+            counts = psum.tile([P, KEY_TILES * 2 * COUNT_COLS], F32, tag="bank")
             for j in range(KEY_TILES):
                 for side, votes in enumerate(both_votes):
                     first = (2 * j + side) * COUNT_COLS
@@ -311,9 +311,6 @@ def tile_crossattention_for_fusion_temporal_pa_kernel(tc, q, k, ki, xs, xis, Wv,
                 if pieces:
                     transpose, empty = pieces[g]()
                 for e in range(PAIR):
-                    if pieces:
-                        transpose(2 * e)
-                        transpose(2 * e + 1)
                     nc.tensor.matmul(
                         score[:],
                         lhsT=qT[unit // STREAMS][:].rearrange("p (g r e) -> p g r e", g=WORD_CHUNKS, e=PAIR)[
@@ -323,6 +320,9 @@ def tile_crossattention_for_fusion_temporal_pa_kernel(tc, q, k, ki, xs, xis, Wv,
                         start=(g == 0 and e == 0),
                         stop=(g == WORD_CHUNKS - 1 and e == PAIR - 1),
                     )
+                    if pieces:
+                        transpose(2 * e)
+                        transpose(2 * e + 1)
                 if pieces:
                     empty()
 
@@ -330,31 +330,34 @@ def tile_crossattention_for_fusion_temporal_pa_kernel(tc, q, k, ki, xs, xis, Wv,
             return lambda: make(*args)
 
         turn_queries(0)
-        piece, view0 = key_pieces(0, (on_vector, on_scalar, on_vector, on_scalar))
+        piece, view0 = key_pieces(0, (on_scalar,) * 4)
+        first = [piece(g) for g in range(WORD_CHUNKS)]
+        for part in range(2):
+            for g in range(WORD_CHUNKS):
+                for j in range(2 * part, 2 * part + 2):
+                    first[g][0](j)
         for g in range(WORD_CHUNKS):
-            run_piece(piece(g))
-        piece, view1 = key_pieces(1, (on_scalar, on_scalar, on_scalar, on_scalar))
+            first[g][1]()
+        piece, view1 = key_pieces(1, (on_scalar,) * 4)
         score_unit(0, view0, [bound(piece, g) for g in range(WORD_CHUNKS)])
         turn_queries(1)
         softmaxes[0] = softmax_start(scores[0])
-        piece, view2 = key_pieces(2, (on_scalar, on_scalar, on_scalar, on_scalar))
+        regroup_weights(0, 0, nc.vector)
+        piece, view2 = key_pieces(2, (on_scalar,) * 4)
         score_unit(1, view1, [bound(piece, g) for g in range(WORD_CHUNKS)])
         softmax_finish(*softmaxes[0])
+        regroup_weights(0, 1, nc.vector)
         softmaxes[1] = softmax_start(scores[1])
-        piece, view3 = key_pieces(3, (on_scalar, on_scalar, on_scalar, on_scalar))
+        piece, view3 = key_pieces(3, (on_scalar,) * 4)
         score_unit(2, view2, [bound(piece, g) for g in range(WORD_CHUNKS)])
-        regroup_weights(0, 0, nc.vector)
-        regroup_weights(0, 1, nc.gpsimd)
-        softmax_finish(*softmaxes[1])
         quantise_weights(0, 0)
-        softmaxes[2] = softmax_start(scores[2])
-        score_unit(3, view3, None)
-        regroup_weights(1, 0, nc.vector)
-        regroup_weights(1, 1, nc.gpsimd)
+        softmax_finish(*softmaxes[1])
         quantise_weights(0, 1)
         votes_of[0] = cast_votes(softmaxes[0][0], softmaxes[1][0])
+        regroup_weights(1, 0, nc.vector)
+        regroup_weights(1, 1, nc.vector)
         quantise_weights(1, 0)
-        softmax_finish(*softmaxes[2])
+        score_unit(3, view3, None)
         run_piece(token_piece(0, 0, on_scalar))
         run_piece(token_piece(0, 1, on_scalar))
         factors_of[0] = count_votes(0, votes_of[0])
@@ -362,24 +365,23 @@ def tile_crossattention_for_fusion_temporal_pa_kernel(tc, q, k, ki, xs, xis, Wv,
         run_piece(token_piece(1, 1, on_scalar))
         quantise_tokens(0)
         quantise_weights(1, 1)
-        softmaxes[3] = softmax_start(scores[3])
         quantise_tokens(1)
-        for step in (2, 3):
-            split_words(step, nc.gpsimd.tensor_copy)
         project(0, factors_of[0])
-        softmax_finish(*softmaxes[3])
+        softmaxes[2] = softmax_start(scores[2])
         for step in (2, 4, 6):
             turn_tokens(step)
             turn_tokens(step + 1)
+            if step == 2:
+                softmaxes[3] = softmax_start(scores[3])
             quantise_tokens(step)
             if step == 2:
-                votes_of[1] = cast_votes(softmaxes[2][0], softmaxes[3][0])
+                softmax_finish(*softmaxes[2])
+                softmax_finish(*softmaxes[3])
             if step == 4:
                 factors_of[1] = count_votes(1, votes_of[1])
             project(step - 1, factors_of[(step - 1) // KEY_TILES])
             quantise_tokens(step + 1)
-            for later in (step + 2, step + 3):
-                if later < 8:
-                    split_words(later, nc.gpsimd.tensor_copy)
+            if step == 2:
+                votes_of[1] = cast_votes(softmaxes[2][0], softmaxes[3][0])
             project(step, factors_of[step // KEY_TILES])
         project(7, factors_of[1], True)

@@ -30,6 +30,10 @@ BANK = 512
 DV_HALVES = DV // BANK
 COUNT_COLS = 32
 SCALE = C**-0.5
+BY_STREAM = [(stream, h) for stream in range(STREAMS) for h in range(DV_HALVES)]
+BY_HALF = [(stream, h) for h in range(DV_HALVES) for stream in range(STREAMS)]
+FIRST_HALF = BY_HALF[:STREAMS]
+SECOND_HALF = BY_HALF[STREAMS:]
 
 FLOPS = 2 * BATCH * 2 * QUERIES * KEYS * C + 2 * BATCH * 2 * KEYS * C * DV
 
@@ -83,8 +87,8 @@ def tile_crossattention_for_fusion_temporal_pa_kernel(tc, q, k, ki, xs, xis, Wv,
         load_keys(1, 1)
         load_queries(1)
         load_keys(2, 1)
-        load_weights(0)
         load_keys(3, 1)
+        load_weights(0)
         load_weights(1)
         for step in range(BATCH * KEY_TILES):
             load_tokens(step)
@@ -260,42 +264,47 @@ def tile_crossattention_for_fusion_temporal_pa_kernel(tc, q, k, ki, xs, xis, Wv,
             )
             return factors
 
-        def project(step, factors, last=False):
+        kept_of = {}
+        mixed_of = {}
+
+        def project(step, bands, stores):
             b, j = divmod(step, KEY_TILES)
+            factors = factors_of[b]
             codes, scales = quantised_of[step]
-            kept = rotating.tile([P, DV], F32, tag="kept", bufs=3)
-            mixed = rotating.tile([P, DV], F32, tag="mixed", bufs=4)
+            if step not in kept_of:
+                kept = rotating.tile([P, DV], F32, tag="kept", bufs=3)
+                mixed = rotating.tile([P, DV], F32, tag="mixed", bufs=4)
+                kept_of[step], mixed_of[step] = kept, mixed
+            kept, mixed = kept_of[step], mixed_of[step]
             out_rows = out[b].rearrange("(p j) d -> p j d", j=KEY_TILES)[:, j, :]
-            pairs = [(stream, h) for stream in range(STREAMS) for h in range(DV_HALVES)]
-            if last:
-                pairs = [(stream, h) for h in range(DV_HALVES) for stream in range(STREAMS)]
-            for stream, h in pairs:
-                    cols = slice(h * BANK, (h + 1) * BANK)
-                    acc = psum.tile([P, BANK], F32, tag="bank")
-                    for g in range(PASSES):
-                        first = (stream * PASSES + g) * P
-                        nc.tensor.matmul_mx(
-                            out=acc[:],
-                            lhsT=codes[:, first : first + P].bitcast(FP8X4),
-                            lhsT_scale=scales[:, first : first + P],
-                            rhs=w_codes[g][:, cols].bitcast(FP8X4),
-                            rhs_scale=w_scales[g][:, cols],
-                            start=(g == 0),
-                            stop=(g == PASSES - 1),
-                        )
-                    if stream == 0:
-                        nc.scalar.activation(
-                            out=kept[:, cols], in_=acc[:], func=ACT.Copy, scale=factors[:, 2 * j : 2 * j + 1]
-                        )
-                    else:
-                        nc.vector.scalar_tensor_tensor(
-                            out=mixed[:, cols],
-                            in0=acc[:],
-                            scalar=factors[:, 2 * j + 1 : 2 * j + 2],
-                            in1=kept[:, cols],
-                            op0=ALU.mult,
-                            op1=ALU.add,
-                        )
+            for stream, h in bands:
+                cols = slice(h * BANK, (h + 1) * BANK)
+                acc = psum.tile([P, BANK], F32, tag="bank")
+                for g in range(PASSES):
+                    first = (stream * PASSES + g) * P
+                    nc.tensor.matmul_mx(
+                        out=acc[:],
+                        lhsT=codes[:, first : first + P].bitcast(FP8X4),
+                        lhsT_scale=scales[:, first : first + P],
+                        rhs=w_codes[g][:, cols].bitcast(FP8X4),
+                        rhs_scale=w_scales[g][:, cols],
+                        start=(g == 0),
+                        stop=(g == PASSES - 1),
+                    )
+                if stream == 0:
+                    nc.scalar.activation(
+                        out=kept[:, cols], in_=acc[:], func=ACT.Copy, scale=factors[:, 2 * j : 2 * j + 1]
+                    )
+                else:
+                    nc.vector.scalar_tensor_tensor(
+                        out=mixed[:, cols],
+                        in0=acc[:],
+                        scalar=factors[:, 2 * j + 1 : 2 * j + 2],
+                        in1=kept[:, cols],
+                        op0=ALU.mult,
+                        op1=ALU.add,
+                    )
+                    if stores:
                         nc.sync.dma_start(out=out_rows[:, cols], in_=mixed[:, cols])
 
         on_scalar, on_vector = nc.scalar.copy, nc.vector.tensor_copy
@@ -307,24 +316,28 @@ def tile_crossattention_for_fusion_temporal_pa_kernel(tc, q, k, ki, xs, xis, Wv,
         def score_unit(unit, view, pieces):
             score = score_psum.tile([P, KEYS], F32, tag="score")
             scores[unit] = score
-            for g in range(WORD_CHUNKS):
-                if pieces:
-                    transpose, empty = pieces[g]()
-                for e in range(PAIR):
+            halves = 2 if pieces else 1
+            half_keys = KEYS // halves
+            chunks = [(g, e) for g in range(WORD_CHUNKS) for e in range(PAIR)]
+            for half in range(halves):
+                keys = slice(half * half_keys, (half + 1) * half_keys)
+                for i, (g, e) in enumerate(chunks):
                     nc.tensor.matmul(
-                        score[:],
+                        score[:, keys],
                         lhsT=qT[unit // STREAMS][:].rearrange("p (g r e) -> p g r e", g=WORD_CHUNKS, e=PAIR)[
                             :, g, :, e
                         ],
-                        rhs=view[:, g, :, e],
-                        start=(g == 0 and e == 0),
-                        stop=(g == WORD_CHUNKS - 1 and e == PAIR - 1),
+                        rhs=view[:, g, keys, e],
+                        start=(i == 0),
+                        stop=(i == len(chunks) - 1),
                     )
                     if pieces:
-                        transpose(2 * e)
-                        transpose(2 * e + 1)
-                if pieces:
-                    empty()
+                        n = half * len(chunks) + i
+                        if n % 4 == 0:
+                            transpose, empty = pieces[n // 4]()
+                        transpose(n % 4)
+                        if n % 4 == 3:
+                            empty()
 
         def bound(make, *args):
             return lambda: make(*args)
@@ -342,21 +355,20 @@ def tile_crossattention_for_fusion_temporal_pa_kernel(tc, q, k, ki, xs, xis, Wv,
         score_unit(0, view0, [bound(piece, g) for g in range(WORD_CHUNKS)])
         turn_queries(1)
         softmaxes[0] = softmax_start(scores[0])
-        regroup_weights(0, 0, nc.vector)
         piece, view2 = key_pieces(2, (on_scalar,) * 4)
         score_unit(1, view1, [bound(piece, g) for g in range(WORD_CHUNKS)])
         softmax_finish(*softmaxes[0])
-        regroup_weights(0, 1, nc.vector)
         softmaxes[1] = softmax_start(scores[1])
         piece, view3 = key_pieces(3, (on_scalar,) * 4)
         score_unit(2, view2, [bound(piece, g) for g in range(WORD_CHUNKS)])
-        quantise_weights(0, 0)
         softmax_finish(*softmaxes[1])
-        quantise_weights(0, 1)
+        regroup_weights(0, 1, nc.scalar)
+        regroup_weights(0, 0, nc.vector)
         votes_of[0] = cast_votes(softmaxes[0][0], softmaxes[1][0])
         regroup_weights(1, 0, nc.vector)
-        regroup_weights(1, 1, nc.vector)
+        quantise_weights(0, 0)
         quantise_weights(1, 0)
+        quantise_weights(0, 1)
         score_unit(3, view3, None)
         run_piece(token_piece(0, 0, on_scalar))
         run_piece(token_piece(0, 1, on_scalar))
@@ -364,24 +376,34 @@ def tile_crossattention_for_fusion_temporal_pa_kernel(tc, q, k, ki, xs, xis, Wv,
         run_piece(token_piece(1, 0, on_scalar))
         run_piece(token_piece(1, 1, on_scalar))
         quantise_tokens(0)
-        quantise_weights(1, 1)
         quantise_tokens(1)
-        project(0, factors_of[0])
+        regroup_weights(1, 1, nc.vector)
+        quantise_weights(1, 1)
+        project(0, FIRST_HALF, True)
+        project(1, FIRST_HALF, True)
+        turn_tokens(2)
+        turn_tokens(3)
         softmaxes[2] = softmax_start(scores[2])
-        for step in (2, 4, 6):
-            turn_tokens(step)
-            turn_tokens(step + 1)
-            if step == 2:
-                softmaxes[3] = softmax_start(scores[3])
-            quantise_tokens(step)
-            if step == 2:
-                softmax_finish(*softmaxes[2])
-                softmax_finish(*softmaxes[3])
-            if step == 4:
-                factors_of[1] = count_votes(1, votes_of[1])
-            project(step - 1, factors_of[(step - 1) // KEY_TILES])
-            quantise_tokens(step + 1)
-            if step == 2:
-                votes_of[1] = cast_votes(softmaxes[2][0], softmaxes[3][0])
-            project(step, factors_of[step // KEY_TILES])
-        project(7, factors_of[1], True)
+        softmaxes[3] = softmax_start(scores[3])
+        quantise_tokens(2)
+        project(0, SECOND_HALF, True)
+        project(1, SECOND_HALF, True)
+        softmax_finish(*softmaxes[2])
+        softmax_finish(*softmaxes[3])
+        quantise_tokens(3)
+        project(2, BY_STREAM, True)
+        turn_tokens(4)
+        turn_tokens(5)
+        votes_of[1] = cast_votes(softmaxes[2][0], softmaxes[3][0])
+        quantise_tokens(4)
+        project(3, BY_STREAM, True)
+        quantise_tokens(5)
+        factors_of[1] = count_votes(1, votes_of[1])
+        project(4, BY_STREAM, True)
+        turn_tokens(6)
+        turn_tokens(7)
+        quantise_tokens(6)
+        project(5, BY_STREAM, True)
+        quantise_tokens(7)
+        project(6, BY_STREAM, True)
+        project(7, BY_HALF, True)

@@ -30,10 +30,10 @@ BANK = 512
 DV_HALVES = DV // BANK
 COUNT_COLS = 32
 SCALE = C**-0.5
-BY_STREAM = [(stream, h) for stream in range(STREAMS) for h in range(DV_HALVES)]
-BY_HALF = [(stream, h) for h in range(DV_HALVES) for stream in range(STREAMS)]
-FIRST_HALF = BY_HALF[:STREAMS]
-SECOND_HALF = BY_HALF[STREAMS:]
+BY_STREAM = [(stream, h * BANK, BANK) for stream in range(STREAMS) for h in range(DV_HALVES)]
+FIRST_HALF = [(stream, 0, BANK) for stream in range(STREAMS)]
+SECOND_HALF = [(stream, BANK, BANK) for stream in range(STREAMS)]
+BY_HALF = FIRST_HALF + [(0, BANK, BANK), (1, BANK, BANK // 2), (1, BANK + BANK // 2, BANK // 2)]
 
 FLOPS = 2 * BATCH * 2 * QUERIES * KEYS * C + 2 * BATCH * 2 * KEYS * C * DV
 
@@ -136,6 +136,14 @@ def tile_crossattention_for_fusion_temporal_pa_kernel(tc, q, k, ki, xs, xis, Wv,
         def transpose_words(bank_cols, words):
             nc.tensor.transpose(bank_cols, words, ident[:])
 
+        idle_operand = resident.tile([P, BANK], BF16, name="idle_operand")
+        nc.vector.memset(idle_operand[:], 0.0)
+
+        def keep_warm(count):
+            bank = psum.tile([P, BANK], F32, tag="bank")
+            for i in range(count):
+                nc.tensor.matmul(bank[:], lhsT=idle_operand[:, :P], rhs=idle_operand[:], start=True, stop=True)
+
         qT = [resident.tile([P, C], BF16, name="qT%d" % b) for b in range(BATCH)]
 
         def turn_queries(b):
@@ -164,7 +172,7 @@ def tile_crossattention_for_fusion_temporal_pa_kernel(tc, q, k, ki, xs, xis, Wv,
             view = kT[:].rearrange("p (g n e) -> p g n e", g=WORD_CHUNKS, e=PAIR)
             return piece, view
 
-        SPLIT = ()
+        SPLIT = (6, 7)
         split_of = {}
 
         def split_words(step, engine):
@@ -277,13 +285,14 @@ def tile_crossattention_for_fusion_temporal_pa_kernel(tc, q, k, ki, xs, xis, Wv,
                 kept_of[step], mixed_of[step] = kept, mixed
             kept, mixed = kept_of[step], mixed_of[step]
             out_rows = out[b].rearrange("(p j) d -> p j d", j=KEY_TILES)[:, j, :]
-            for stream, h in bands:
-                cols = slice(h * BANK, (h + 1) * BANK)
-                acc = psum.tile([P, BANK], F32, tag="bank")
+            for stream, first_col, width in bands:
+                cols = slice(first_col, first_col + width)
+                bank = psum.tile([P, BANK], F32, tag="bank")
+                acc = bank[:, :width]
                 for g in range(PASSES):
                     first = (stream * PASSES + g) * P
                     nc.tensor.matmul_mx(
-                        out=acc[:],
+                        out=acc,
                         lhsT=codes[:, first : first + P].bitcast(FP8X4),
                         lhsT_scale=scales[:, first : first + P],
                         rhs=w_codes[g][:, cols].bitcast(FP8X4),
@@ -293,12 +302,12 @@ def tile_crossattention_for_fusion_temporal_pa_kernel(tc, q, k, ki, xs, xis, Wv,
                     )
                 if stream == 0:
                     nc.scalar.activation(
-                        out=kept[:, cols], in_=acc[:], func=ACT.Copy, scale=factors[:, 2 * j : 2 * j + 1]
+                        out=kept[:, cols], in_=acc, func=ACT.Copy, scale=factors[:, 2 * j : 2 * j + 1]
                     )
                 else:
                     nc.vector.scalar_tensor_tensor(
                         out=mixed[:, cols],
-                        in0=acc[:],
+                        in0=acc,
                         scalar=factors[:, 2 * j + 1 : 2 * j + 2],
                         in1=kept[:, cols],
                         op0=ALU.mult,
@@ -372,6 +381,7 @@ def tile_crossattention_for_fusion_temporal_pa_kernel(tc, q, k, ki, xs, xis, Wv,
         score_unit(3, view3, None)
         run_piece(token_piece(0, 0, on_scalar))
         run_piece(token_piece(0, 1, on_scalar))
+        keep_warm(2)
         factors_of[0] = count_votes(0, votes_of[0])
         run_piece(token_piece(1, 0, on_scalar))
         run_piece(token_piece(1, 1, on_scalar))
@@ -398,6 +408,8 @@ def tile_crossattention_for_fusion_temporal_pa_kernel(tc, q, k, ki, xs, xis, Wv,
         quantise_tokens(4)
         project(3, BY_STREAM, True)
         quantise_tokens(5)
+        split_words(6, nc.scalar.copy)
+        split_words(7, nc.vector.tensor_copy)
         factors_of[1] = count_votes(1, votes_of[1])
         project(4, BY_STREAM, True)
         turn_tokens(6)

@@ -103,14 +103,14 @@ def tile_crossattention_for_fusion_temporal_pa_kernel(tc, q, k, ki, xs, xis, Wv,
         nc.scalar.activation(out=one[:], in_=zero[:], func=ACT.Exp)
 
         w_grouped = [
-            resident.tile([P, DV * PACK], BF16, name="w_grouped%d" % g, align_bytes=64)
+            resident.tile([P, DV * PACK], BF16, name="w_grouped%d" % g, align_bytes=256)
             for g in range(PASSES)
         ]
         w_codes = [
-            resident.tile([P, DV], U32, name="w_codes%d" % g, align_bytes=64) for g in range(PASSES)
+            resident.tile([P, DV], U32, name="w_codes%d" % g, align_bytes=256) for g in range(PASSES)
         ]
         w_scales = [
-            resident.tile([P, DV], U8, name="w_scales%d" % g, align_bytes=64) for g in range(PASSES)
+            resident.tile([P, DV], U8, name="w_scales%d" % g, align_bytes=256) for g in range(PASSES)
         ]
 
         def regroup_weights(g, h, engine):
@@ -191,7 +191,7 @@ def tile_crossattention_for_fusion_temporal_pa_kernel(tc, q, k, ki, xs, xis, Wv,
                 :, stream * WORDS : (stream + 1) * WORDS
             ]
             if stream == 0:
-                grouped = rotating.tile([P, STREAMS * C], BF16, tag="grouped", align_bytes=64, bufs=4)
+                grouped = rotating.tile([P, STREAMS * C], BF16, tag="grouped", align_bytes=256, bufs=4)
                 grouped_of[step] = grouped
             grouped = grouped_of[step]
             bank = psum.tile([P, BANK], F32, tag="bank")
@@ -223,8 +223,8 @@ def tile_crossattention_for_fusion_temporal_pa_kernel(tc, q, k, ki, xs, xis, Wv,
             run_piece(token_piece(step, 1, nc.scalar.copy))
 
         def quantise_tokens(step):
-            codes = rotating.tile([P, STREAMS * PASSES * P], U32, tag="codes", align_bytes=64, bufs=4)
-            scales = rotating.tile([P, STREAMS * PASSES * P], U8, tag="scales", align_bytes=64, bufs=4)
+            codes = rotating.tile([P, STREAMS * PASSES * P], U32, tag="codes", align_bytes=256, bufs=4)
+            scales = rotating.tile([P, STREAMS * PASSES * P], U8, tag="scales", align_bytes=256, bufs=4)
             nc.vector.quantize_mx(
                 out=codes[:].bitcast(FP8X4), scales=scales[:], in_=grouped_of[step][:]
             )

from contextlib import ExitStack

import concourse.mybir as mybir
from concourse.masks import make_identity

BF16 = mybir.dt.bfloat16
F32 = mybir.dt.float32
U32 = mybir.dt.uint32
U8 = mybir.dt.uint8
FP8X4 = mybir.dt.float8_e4m3fn_x4
ALU = mybir.AluOpType
ACT = mybir.ActivationFunctionType
AXIS = mybir.AxisListType

P = 128
BATCH = 2
STREAMS = 2
QUERIES = 128
KEYS = 512
C = 1024
DV = 1024
KEY_TILES = KEYS // P
HALF_TILES = KEY_TILES // 2
PAIR = 2
WORDS = C // PAIR
WORD_CHUNKS = WORDS // P
PACK = 4
PASSES = C // (P * PACK)
BANK = 512
DV_HALVES = DV // BANK
COUNT_COLS = 32
SCALE = C**-0.5
BY_STREAM = [(stream, h * BANK, BANK) for stream in range(STREAMS) for h in range(DV_HALVES)]
FIRST_HALF = [(stream, 0, BANK) for stream in range(STREAMS)]
SECOND_HALF = [(stream, BANK, BANK) for stream in range(STREAMS)]
BY_HALF = FIRST_HALF + [(0, BANK, BANK), (1, BANK, BANK // 2), (1, BANK + BANK // 2, BANK // 2)]

FLOPS = 2 * BATCH * 2 * QUERIES * KEYS * C + 2 * BATCH * 2 * KEYS * C * DV


def tile_crossattention_for_fusion_temporal_pa_kernel(tc, q, k, ki, xs, xis, Wv, out):
    nc = tc.nc
    with ExitStack() as ctx:
        resident = ctx.enter_context(tc.tile_pool(name="resident", bufs=1))
        rotating = ctx.enter_context(tc.tile_pool(name="rotating", bufs=2))
        small = ctx.enter_context(tc.tile_pool(name="small", bufs=4))
        score_psum = ctx.enter_context(tc.psum_pool(name="score_psum", bufs=2))
        psum = ctx.enter_context(tc.psum_pool(name="psum", bufs=6))
        ctx.enter_context(tc.manual_schedule())

        q_sb = [resident.tile([P, C], BF16, name="q_sb%d" % b) for b in range(BATCH)]
        keys_sb = [
            resident.tile([P, KEY_TILES * C], BF16, name="keys_sb%d" % u)
            for u in range(BATCH * STREAMS)
        ]
        tokens_sb = [
            resident.tile([P, STREAMS * C], BF16, name="tokens_sb%d" % step)
            for step in range(BATCH * KEY_TILES)
        ]
        w_raw = [resident.tile([P, PACK * DV], BF16, name="w_raw%d" % g) for g in range(PASSES)]

        def load_queries(b):
            nc.sync.dma_start(out=q_sb[b][:], in_=q[b])

        def load_keys(unit, parts):
            b, stream = divmod(unit, STREAMS)
            rows = (k, ki)[stream][b].rearrange("(p j) c -> p (j c)", j=KEY_TILES)
            width = KEY_TILES * C // parts
            for i in range(parts):
                cols = slice(i * width, (i + 1) * width)
                nc.sync.dma_start(out=keys_sb[unit][:, cols], in_=rows[:, cols])

        def load_tokens(step):
            b, j = divmod(step, KEY_TILES)
            for stream, x in enumerate((xs, xis)):
                nc.sync.dma_start(
                    out=tokens_sb[step][:, stream * C : (stream + 1) * C],
                    in_=x[b].rearrange("(p j) c -> p j c", j=KEY_TILES)[:, j, :],
                )

        def load_weights(g):
            rows = Wv[g * P * PACK : (g + 1) * P * PACK, :]
            nc.sync.dma_start(out=w_raw[g][:], in_=rows.rearrange("(p t) d -> p (t d)", t=PACK))

        load_queries(0)
        load_keys(0, 2)
        load_keys(1, 1)
        load_queries(1)
        load_keys(2, 1)
        load_keys(3, 1)
        load_weights(0)
        load_weights(1)
        for step in range(BATCH * KEY_TILES):
            load_tokens(step)

        ident = resident.tile([P, P], F32, name="ident")
        make_identity(nc, ident[:])
        vote_share = resident.tile([P, COUNT_COLS], BF16, name="vote_share")
        nc.vector.memset(vote_share[:], 1.0 / QUERIES)
        zero = small.tile([P, 1], F32, tag="zero")
        nc.vector.memset(zero[:], 0.0)
        one = small.tile([P, 1], F32, tag="one")
        nc.scalar.activation(out=one[:], in_=zero[:], func=ACT.Exp)

        w_grouped = [
            resident.tile([P, DV * PACK], BF16, name="w_grouped%d" % g, align_bytes=256)
            for g in range(PASSES)
        ]
        w_codes = [
            resident.tile([P, DV], U32, name="w_codes%d" % g, align_bytes=256) for g in range(PASSES)
        ]
        w_scales = [
            resident.tile([P, DV], U8, name="w_scales%d" % g, align_bytes=256) for g in range(PASSES)
        ]

        def regroup_weights(g, h, engine):
            cols = slice(h * BANK, (h + 1) * BANK)
            grouped = w_grouped[g][:].rearrange("p (d t) -> p d t", t=PACK)[:, cols, :]
            raw = w_raw[g][:].rearrange("p (t d) -> p t d", t=PACK)[:, :, cols]
            if engine is nc.gpsimd:
                engine.tensor_copy(out=grouped, in_=raw.rearrange("p t d -> p d t"))
            else:
                (engine.copy if engine is nc.scalar else engine.tensor_copy)(
                    out=grouped.rearrange("p (c i) t -> p c t i", i=4),
                    in_=raw.rearrange("p t (c i) -> p c t i", i=4),
                )

        def quantise_weights(g, h):
            cols = slice(h * BANK, (h + 1) * BANK)
            nc.vector.quantize_mx(
                out=w_codes[g][:, cols].bitcast(FP8X4),
                scales=w_scales[g][:, cols],
                in_=w_grouped[g][:, h * BANK * PACK : (h + 1) * BANK * PACK],
            )

        def transpose_words(bank_cols, words):
            nc.tensor.transpose(bank_cols, words, ident[:])

        idle_operand = resident.tile([P, BANK], BF16, name="idle_operand")
        nc.vector.memset(idle_operand[:], 0.0)

        def keep_warm(count):
            bank = psum.tile([P, BANK], F32, tag="bank")
            for i in range(count):
                nc.tensor.matmul(bank[:], lhsT=idle_operand[:, :P], rhs=idle_operand[:], start=True, stop=True)

        qT = [resident.tile([P, C], BF16, name="qT%d" % b) for b in range(BATCH)]

        def turn_queries(b):
            bank = psum.tile([P, BANK], F32, tag="bank")
            words = q_sb[b][:].bitcast(F32)
            for g in range(WORD_CHUNKS):
                transpose_words(bank[:, g * P : (g + 1) * P], words[:, g * P : (g + 1) * P])
            nc.scalar.copy(out=qT[b][:].bitcast(F32), in_=bank[:])

        def key_pieces(unit, engines):
            words = keys_sb[unit][:].bitcast(F32).rearrange("p (j w) -> p j w", j=KEY_TILES)
            kT = rotating.tile([P, WORD_CHUNKS * PAIR * BANK], BF16, tag="kT")
            kT_words = kT[:].bitcast(F32)

            def piece(g):
                bank = psum.tile([P, BANK], F32, tag="bank")

                def transpose(j):
                    transpose_words(bank[:, j * P : (j + 1) * P], words[:, j, g * P : (g + 1) * P])

                def empty():
                    engines[g](out=kT_words[:, g * BANK : (g + 1) * BANK], in_=bank[:])

                return transpose, empty

            view = kT[:].rearrange("p (g n e) -> p g n e", g=WORD_CHUNKS, e=PAIR)
            return piece, view

        SPLIT = (6, 7)
        split_of = {}

        def split_words(step, engine):
            split = rotating.tile([P, STREAMS * C], BF16, tag="split", bufs=4)
            split_of[step] = split
            engine(
                out=split[:].bitcast(F32).rearrange("p (n u w) -> p n u w", n=STREAMS, u=2),
                in_=tokens_sb[step][:].bitcast(F32).rearrange("p (n w u) -> p n u w", n=STREAMS, u=2),
            )

        grouped_of = {}
        quantised_of = {}

        def token_piece(step, stream, engine):
            words = (split_of if step in SPLIT else tokens_sb)[step][:].bitcast(F32)[
                :, stream * WORDS : (stream + 1) * WORDS
            ]
            if stream == 0:
                grouped = rotating.tile([P, STREAMS * C], BF16, tag="grouped", align_bytes=256, bufs=4)
                grouped_of[step] = grouped
            grouped = grouped_of[step]
            bank = psum.tile([P, BANK], F32, tag="bank")

            def transpose(i):
                g, u = divmod(i, 2)
                transpose_words(
                    bank[:, i * P : (i + 1) * P], (words[:, 2 * P * g + u : 2 * P * (g + 1) : 2] if step not in SPLIT else words[:, u * 2 * P + g * P : u * 2 * P + (g + 1) * P])
                )

            def empty():
                engine(
                    out=grouped[:].bitcast(F32)[:, stream * WORDS : (stream + 1) * WORDS].rearrange(
                        "p (g n u) -> p g n u", g=PASSES, u=2
                    ),
                    in_=bank[:].rearrange("p (g u n) -> p g n u", g=PASSES, u=2),
                )

            return transpose, empty

        def run_piece(piece):
            transpose, empty = piece
            for i in range(4):
                transpose(i)
            empty()

        def turn_tokens(step):
            run_piece(token_piece(step, 0, nc.scalar.copy))
            run_piece(token_piece(step, 1, nc.scalar.copy))

        def quantise_tokens(step):
            codes = rotating.tile([P, STREAMS * PASSES * P], U32, tag="codes", align_bytes=256, bufs=4)
            scales = rotating.tile([P, STREAMS * PASSES * P], U8, tag="scales", align_bytes=256, bufs=4)
            nc.vector.quantize_mx(
                out=codes[:].bitcast(FP8X4), scales=scales[:], in_=grouped_of[step][:]
            )
            quantised_of[step] = (codes, scales)

        def softmax_start(score):
            top = small.tile([P, 1], F32, tag="top")
            nc.vector.reduce_max(out=top[:], in_=score[:], axis=AXIS.X)
            shift = small.tile([P, 1], F32, tag="shift")
            nc.vector.tensor_scalar_mul(out=shift[:], in0=top[:], scalar1=-SCALE)
            attn = rotating.tile([P, KEYS], F32, tag="attn", bufs=4)
            total = small.tile([P, 1], F32, tag="total")
            nc.scalar.activation(
                out=attn[:], in_=score[:], func=ACT.Exp, bias=shift[:], scale=SCALE, accum_out=total[:]
            )
            return attn, total

        def softmax_finish(attn, total):
            inverse = small.tile([P, 1], F32, tag="inverse")
            nc.vector.reciprocal(out=inverse[:], in_=total[:])
            nc.vector.tensor_scalar_mul(out=attn[:], in0=attn[:], scalar1=inverse[:])

        def cast_votes(aw, awi):
            not_less = rotating.tile([P, KEYS], BF16, tag="not_less")
            nc.vector.tensor_tensor(out=not_less[:], in0=aw[:], in1=awi[:], op=ALU.is_ge)
            not_more = rotating.tile([P, KEYS], BF16, tag="not_more")
            nc.vector.tensor_tensor(out=not_more[:], in0=aw[:], in1=awi[:], op=ALU.is_le)
            return not_less, not_more

        def count_votes(b, both_votes):
            counts = psum.tile([P, KEY_TILES * 2 * COUNT_COLS], F32, tag="bank")
            for j in range(KEY_TILES):
                for side, votes in enumerate(both_votes):
                    first = (2 * j + side) * COUNT_COLS
                    nc.tensor.matmul(
                        counts[:, first : first + COUNT_COLS],
                        lhsT=votes[:, j * P : (j + 1) * P],
                        rhs=vote_share[:],
                        start=True,
                        stop=True,
                    )
            factors = resident.tile([P, KEY_TILES * 2], F32, name="factors%d" % b)
            nc.vector.tensor_copy(
                out=factors[:], in_=counts[:].rearrange("p (i n) -> p i n", n=COUNT_COLS)[:, :, 0]
            )
            return factors

        kept_of = {}
        mixed_of = {}

        def project(step, bands, stores):
            b, j = divmod(step, KEY_TILES)
            factors = factors_of[b]
            codes, scales = quantised_of[step]
            if step not in kept_of:
                kept = rotating.tile([P, DV], F32, tag="kept", bufs=3)
                mixed = rotating.tile([P, DV], F32, tag="mixed", bufs=4)
                kept_of[step], mixed_of[step] = kept, mixed
            kept, mixed = kept_of[step], mixed_of[step]
            out_rows = out[b].rearrange("(p j) d -> p j d", j=KEY_TILES)[:, j, :]
            for stream, first_col, width in bands:
                cols = slice(first_col, first_col + width)
                bank = psum.tile([P, BANK], F32, tag="bank")
                acc = bank[:, :width]
                for g in range(PASSES):
                    first = (stream * PASSES + g) * P
                    nc.tensor.matmul_mx(
                        out=acc,
                        lhsT=codes[:, first : first + P].bitcast(FP8X4),
                        lhsT_scale=scales[:, first : first + P],
                        rhs=w_codes[g][:, cols].bitcast(FP8X4),
                        rhs_scale=w_scales[g][:, cols],
                        start=(g == 0),
                        stop=(g == PASSES - 1),
                    )
                if stream == 0:
                    nc.scalar.activation(
                        out=kept[:, cols], in_=acc, func=ACT.Copy, scale=factors[:, 2 * j : 2 * j + 1]
                    )
                else:
                    nc.vector.scalar_tensor_tensor(
                        out=mixed[:, cols],
                        in0=acc,
                        scalar=factors[:, 2 * j + 1 : 2 * j + 2],
                        in1=kept[:, cols],
                        op0=ALU.mult,
                        op1=ALU.add,
                    )
                    if stores:
                        nc.sync.dma_start(out=out_rows[:, cols], in_=mixed[:, cols])

        on_scalar, on_vector = nc.scalar.copy, nc.vector.tensor_copy
        scores = {}
        softmaxes = {}
        votes_of = {}
        factors_of = {}

        def score_unit(unit, view, pieces):
            score = score_psum.tile([P, KEYS], F32, tag="score")
            scores[unit] = score
            halves = 2 if pieces else 1
            half_keys = KEYS // halves
            chunks = [(g, e) for g in range(WORD_CHUNKS) for e in range(PAIR)]
            for half in range(halves):
                keys = slice(half * half_keys, (half + 1) * half_keys)
                for i, (g, e) in enumerate(chunks):
                    nc.tensor.matmul(
                        score[:, keys],
                        lhsT=qT[unit // STREAMS][:].rearrange("p (g r e) -> p g r e", g=WORD_CHUNKS, e=PAIR)[
                            :, g, :, e
                        ],
                        rhs=view[:, g, keys, e],
                        start=(i == 0),
                        stop=(i == len(chunks) - 1),
                    )
                    if pieces:
                        n = half * len(chunks) + i
                        if n % 4 == 0:
                            transpose, empty = pieces[n // 4]()
                        transpose(n % 4)
                        if n % 4 == 3:
                            empty()

        def bound(make, *args):
            return lambda: make(*args)

        turn_queries(0)
        piece, view0 = key_pieces(0, (on_scalar,) * 4)
        first = [piece(g) for g in range(WORD_CHUNKS)]
        for part in range(2):
            for g in range(WORD_CHUNKS):
                for j in range(2 * part, 2 * part + 2):
                    first[g][0](j)
        for g in range(WORD_CHUNKS):
            first[g][1]()
        piece, view1 = key_pieces(1, (on_scalar,) * 4)
        score_unit(0, view0, [bound(piece, g) for g in range(WORD_CHUNKS)])
        turn_queries(1)
        softmaxes[0] = softmax_start(scores[0])
        piece, view2 = key_pieces(2, (on_scalar,) * 4)
        score_unit(1, view1, [bound(piece, g) for g in range(WORD_CHUNKS)])
        softmax_finish(*softmaxes[0])
        softmaxes[1] = softmax_start(scores[1])
        piece, view3 = key_pieces(3, (on_scalar,) * 4)
        score_unit(2, view2, [bound(piece, g) for g in range(WORD_CHUNKS)])
        softmax_finish(*softmaxes[1])
        regroup_weights(0, 1, nc.scalar)
        regroup_weights(0, 0, nc.vector)
        votes_of[0] = cast_votes(softmaxes[0][0], softmaxes[1][0])
        regroup_weights(1, 0, nc.vector)
        quantise_weights(0, 0)
        quantise_weights(1, 0)
        quantise_weights(0, 1)
        score_unit(3, view3, None)
        run_piece(token_piece(0, 0, on_scalar))
        run_piece(token_piece(0, 1, on_scalar))
        keep_warm(2)
        factors_of[0] = count_votes(0, votes_of[0])
        run_piece(token_piece(1, 0, on_scalar))
        run_piece(token_piece(1, 1, on_scalar))
        quantise_tokens(0)
        quantise_tokens(1)
        regroup_weights(1, 1, nc.vector)
        quantise_weights(1, 1)
        project(0, FIRST_HALF, True)
        project(1, FIRST_HALF, True)
        turn_tokens(2)
        turn_tokens(3)
        softmaxes[2] = softmax_start(scores[2])
        softmaxes[3] = softmax_start(scores[3])
        quantise_tokens(2)
        project(0, SECOND_HALF, True)
        project(1, SECOND_HALF, True)
        softmax_finish(*softmaxes[2])
        softmax_finish(*softmaxes[3])
        quantise_tokens(3)
        project(2, BY_STREAM, True)
        turn_tokens(4)
        turn_tokens(5)
        votes_of[1] = cast_votes(softmaxes[2][0], softmaxes[3][0])
        quantise_tokens(4)
        project(3, BY_STREAM, True)
        quantise_tokens(5)
        split_words(6, nc.scalar.copy)
        split_words(7, nc.vector.tensor_copy)
        factors_of[1] = count_votes(1, votes_of[1])
        project(4, BY_STREAM, True)
        turn_tokens(6)
        turn_tokens(7)
        quantise_tokens(6)
        project(5, BY_STREAM, True)
        quantise_tokens(7)
        project(6, BY_STREAM, True)
        project(7, BY_HALF, True)
